import numpy as np
import ml_dtypes


def mxq(x, axis, fmt="e4m3"):
    dtype, down = {"e4m3": (ml_dtypes.float8_e4m3fn, 7), "e5m2": (ml_dtypes.float8_e5m2, 14)}[fmt]
    v = np.moveaxis(np.asarray(x, np.float32).astype(ml_dtypes.bfloat16).astype(np.float64), axis, -1)
    blocks = v.reshape(v.shape[:-1] + (-1, 32))
    amax = np.abs(blocks).max(-1, keepdims=True)
    byte = np.maximum(np.where(amax > 0, np.frexp(amax)[1] - 1 + 127, 0) - down, 1)
    scale = np.exp2(byte - 127.0)
    codes = (blocks / scale).astype(np.float32).astype(dtype).astype(np.float64)
    return np.moveaxis((codes * scale).reshape(v.shape), -1, axis)


WIDE = False


def mx_kscale(k):
    if not WIDE:
        return np.ones(k)
    levels = np.array([10, -10, 5, -5, 0])
    a = np.random.permutation(np.resize(levels, k // 512 * 4)).reshape(k // 512, 4)
    idx = np.arange(k)
    return np.exp2(a[idx // 512, idx % 128 // 32])


BF16 = ml_dtypes.bfloat16


def bf(x):
    return np.asarray(x, np.float32).astype(BF16)


def f64(x):
    return np.asarray(x).astype(np.float64)


B, S, V, E, M = 4096, 16, 256, 512, 512


def setup_inputs():
    s, t = mx_kscale(E), mx_kscale(M)
    return {"y2": bf(np.maximum(np.random.standard_normal((B, E)), 0.0) * s),
            "first": bf(np.random.standard_normal((B, M)) * 0.4 * t),
            "w_second": bf(np.random.standard_normal((M, E)) * 1.4 / np.sqrt(E) / s[None, :]),
            "b_second": bf(np.random.standard_normal(M) * 0.3),
            "w_int": bf(np.random.standard_normal((M, E)) * 1.4 / np.sqrt(E) / s[None, :] * t[:, None]),
            "b_int": bf(np.random.standard_normal(M) * 0.3 * t),
            "w_out": bf(np.random.standard_normal((V, M)) / np.sqrt(M) / t[None, :]),
            "b_out": bf(np.random.standard_normal(V) * 0.3)}


def reference(y2, first, w_second, b_second, w_int, b_int, w_out, b_out):
    y2q = mxq(f64(y2), 1, "e4m3")
    second = np.maximum((y2q @ mxq(f64(w_second), 1, "e4m3").T) + f64(b_second), 0.0)
    inter = np.maximum((y2q @ mxq(f64(w_int), 1, "e4m3").T) + f64(b_int), 0.0)
    z = second * f64(first) + inter
    return (mxq(z, 1, "e4m3") @ mxq(f64(w_out), 1, "e4m3").T) + f64(b_out)

@@ -1,0 +1,212 @@
+from contextlib import ExitStack
+
+import concourse.mybir as mybir
+from concourse.masks import make_identity
+
+F32 = mybir.dt.float32
+BF16 = mybir.dt.bfloat16
+U32 = mybir.dt.uint32
+U8 = mybir.dt.uint8
+FP8X4 = mybir.dt.float8_e4m3fn_x4
+RELU = mybir.ActivationFunctionType.Relu
+MULT = mybir.AluOpType.mult
+ADD = mybir.AluOpType.add
+
+P = 128
+PACK = 4
+K = P * PACK
+BATCH, V = 4096, 256
+GROUP = 512
+CHUNKS = GROUP // P
+HALF = GROUP // 2
+N_GROUPS = BATCH // GROUP
+
+FLOPS = 2 * BATCH * K * (K + K + V)
+
+
+def tile_smcrossbaby_1_pb_t_kernel(
+    tc, y2, first, w_second, b_second, w_int, b_int, w_out, b_out, out
+):
+    nc = tc.nc
+    with ExitStack() as ctx:
+        keep = ctx.enter_context(tc.tile_pool(name="keep", bufs=1))
+        work = ctx.enter_context(tc.tile_pool(name="work", bufs=2))
+        psum_words = ctx.enter_context(tc.psum_pool(name="psum_words", bufs=2))
+        psum_acc = ctx.enter_context(tc.psum_pool(name="psum_acc", bufs=3))
+        psum_out = ctx.enter_context(tc.psum_pool(name="psum_out", bufs=1))
+
+        ident = keep.tile([P, P], F32)
+        make_identity(nc, ident[:])
+
+        y_rows = y2.rearrange("(g p j) k -> g p j k", p=P, j=CHUNKS)
+        f_rows = first.rearrange("(g p j) m -> g p j m", p=P, j=CHUNKS)
+        out_rows = out.rearrange("(g p j) v -> g p j v", p=P, j=CHUNKS)
+        y_sb = [keep.tile([P, CHUNKS, K], BF16, name="y_sb%d" % g) for g in range(N_GROUPS)]
+        f_sb = [keep.tile([P, CHUNKS, K], BF16, name="f_sb%d" % g) for g in range(N_GROUPS)]
+        ws_sb = keep.tile([P, PACK, K], BF16)
+        wi_sb = keep.tile([P, PACK, K], BF16)
+        wo_sb = keep.tile([P, V // P, K], BF16)
+        nc.sync.dma_start(out=y_sb[0][:], in_=y_rows[0])
+        nc.sync.dma_start(
+            out=ws_sb[:].rearrange("p (u e) k -> p u e k", e=2),
+            in_=w_second.rearrange("(u p e) k -> p u e k", u=2, e=2),
+        )
+        nc.sync.dma_start(
+            out=wi_sb[:].rearrange("p (u e) k -> p u e k", e=2),
+            in_=w_int.rearrange("(u p e) k -> p u e k", u=2, e=2),
+        )
+        nc.sync.dma_start(out=f_sb[0][:], in_=f_rows[0])
+        nc.sync.dma_start(out=wo_sb[:], in_=w_out.rearrange("(c p) m -> p c m", p=P))
+        for g in range(1, N_GROUPS):
+            nc.sync.dma_start(out=y_sb[g][:], in_=y_rows[g])
+            nc.sync.dma_start(out=f_sb[g][:], in_=f_rows[g])
+
+        bs_bf = keep.tile([P, PACK], BF16)
+        bi_bf = keep.tile([P, PACK], BF16)
+        bout_bf = keep.tile([P, V], BF16)
+        bias = keep.tile([P, 2, PACK], F32)
+        for which, (b_bf, b_dram) in enumerate(((bs_bf, b_second), (bi_bf, b_int))):
+            nc.scalar.dma_start(
+                out=b_bf[:].rearrange("p (u e) -> p u e", e=2),
+                in_=b_dram.rearrange("(u p e) -> p u e", u=2, e=2),
+            )
+            nc.vector.tensor_copy(out=bias[:, which, :], in_=b_bf[:])
+        nc.scalar.dma_start(out=bout_bf[:], in_=b_out.partition_broadcast(P))
+        bout = keep.tile([P, 2, V], F32)
+        for c in range(2):
+            nc.vector.tensor_copy(out=bout[:, c, :], in_=bout_bf[:])
+
+        def words_onto_partitions(bank, chunk_a, chunk_b):
+            for c, chunk in enumerate((chunk_a, chunk_b)):
+                for u in range(2):
+                    nc.tensor.transpose(
+                        bank[:, u, c * P : (c + 1) * P],
+                        chunk.bitcast(F32)[:, u * P : (u + 1) * P],
+                        ident[:],
+                    )
+
+        def grouped_words(grouped, first_col, n_cols):
+            view = grouped[:].bitcast(F32).rearrange("p (c u) -> p c u", u=2)
+            return view[:, first_col : first_col + n_cols, :]
+
+        def quantise_weight(w_sb, n_chunks, name):
+            cols = n_chunks * P
+            grouped = keep.tile([P, cols * PACK], BF16, align_bytes=64, name=name + "_grouped")
+            for pair in range(n_chunks // 2):
+                bank = psum_words.tile([P, 2, 2 * P], F32, tag="y_words")
+                words_onto_partitions(bank, w_sb[:, 2 * pair, :], w_sb[:, 2 * pair + 1, :])
+                nc.vector.tensor_copy(
+                    out=grouped_words(grouped, pair * 2 * P, 2 * P),
+                    in_=bank[:].rearrange("p u c -> p c u"),
+                )
+            codes = keep.tile([P, cols], U32, align_bytes=64, name=name + "_codes")
+            scales = keep.tile([P, cols], U8, align_bytes=64, name=name + "_scales")
+            nc.vector.quantize_mx(out=codes[:].bitcast(FP8X4), scales=scales[:], in_=grouped[:])
+            return codes, scales
+
+        y_codes = [keep.tile([P, GROUP], U32, align_bytes=64, name="y_codes%d" % g) for g in range(N_GROUPS)]
+        y_scales = [keep.tile([P, GROUP], U8, align_bytes=64, name="y_scales%d" % g) for g in range(N_GROUPS)]
+
+        def quantise_y(g):
+            y_grouped = work.tile([P, GROUP * PACK], BF16, align_bytes=64)
+            for h in range(2):
+                y_words = psum_words.tile([P, 2, HALF], F32)
+                words_onto_partitions(y_words, y_sb[g][:, 2 * h, :], y_sb[g][:, 2 * h + 1, :])
+                nc.scalar.copy(
+                    out=grouped_words(y_grouped, h * HALF, HALF),
+                    in_=y_words[:].rearrange("p u c -> p c u"),
+                )
+            nc.vector.quantize_mx(
+                out=y_codes[g][:].bitcast(FP8X4), scales=y_scales[g][:], in_=y_grouped[:]
+            )
+
+        def transpose_first(g):
+            banks = []
+            for h in range(2):
+                f_words = psum_words.tile([P, 2, HALF], F32)
+                words_onto_partitions(f_words, f_sb[g][:, 2 * h, :], f_sb[g][:, 2 * h + 1, :])
+                banks.append(f_words)
+            return banks
+
+        def relu_of_product(g, codes, scales, which, result):
+            for t in range(PACK):
+                acc = psum_acc.tile([P, GROUP], F32)
+                nc.tensor.matmul_mx(
+                    out=acc[:],
+                    lhsT=codes[:, t * P : (t + 1) * P].bitcast(FP8X4),
+                    lhsT_scale=scales[:, t * P : (t + 1) * P],
+                    rhs=y_codes[g][:].bitcast(FP8X4),
+                    rhs_scale=y_scales[g][:],
+                    start=True,
+                    stop=True,
+                )
+                nc.scalar.activation(
+                    out=result[:, t, :], in_=acc[:], func=RELU, bias=bias[:, which, t : t + 1], scale=1.0
+                )
+
+        def gate_and_quantise(second, inter, f_banks):
+            z_grouped = work.tile([P, GROUP, PACK], BF16, align_bytes=64)
+            product = work.tile([P, GROUP, PACK], F32)
+            for h in range(2):
+                cols = slice(h * HALF, (h + 1) * HALF)
+                nc.vector.tensor_tensor(
+                    out=product[:, cols, :].rearrange("p b (u e) -> p b u e", e=2),
+                    in0=second[:, :, cols].rearrange("p (u e) b -> p b u e", e=2),
+                    in1=f_banks[h][:].bitcast(BF16).rearrange("p u (b e) -> p b u e", e=2),
+                    op=MULT,
+                )
+            for h in range(2):
+                cols = slice(h * HALF, (h + 1) * HALF)
+                nc.vector.tensor_tensor(
+                    out=z_grouped[:, cols, :],
+                    in0=product[:, cols, :],
+                    in1=inter[:, :, cols].rearrange("p t b -> p b t"),
+                    op=ADD,
+                )
+            z_codes = work.tile([P, GROUP], U32, align_bytes=64)
+            z_scales = work.tile([P, GROUP], U8, align_bytes=64)
+            nc.vector.quantize_mx(
+                out=z_codes[:].bitcast(FP8X4),
+                scales=z_scales[:],
+                in_=z_grouped[:].rearrange("p b t -> p (b t)"),
+            )
+            return z_codes, z_scales
+
+        def output_head(g, z_codes, z_scales):
+            out_sb = work.tile([P, CHUNKS, V], F32)
+            for pair in range(CHUNKS // 2):
+                head = psum_out.tile([P, 2, V], F32)
+                for c in range(2):
+                    j = 2 * pair + c
+                    nc.tensor.matmul_mx(
+                        out=head[:, c, :],
+                        lhsT=z_codes[:, j * P : (j + 1) * P].bitcast(FP8X4),
+                        lhsT_scale=z_scales[:, j * P : (j + 1) * P],
+                        rhs=wo_codes[:].bitcast(FP8X4),
+                        rhs_scale=wo_scales[:],
+                        start=True,
+                        stop=True,
+                    )
+                nc.vector.tensor_tensor(
+                    out=out_sb[:, 2 * pair : 2 * pair + 2, :], in0=head[:], in1=bout[:], op=ADD
+                )
+            nc.sync.dma_start(out=out_rows[g], in_=out_sb[:])
+
+        quantise_y(0)
+        ws_codes, ws_scales = quantise_weight(ws_sb, PACK, "ws")
+        wi_codes, wi_scales = quantise_weight(wi_sb, PACK, "wi")
+        wo_codes, wo_scales = quantise_weight(wo_sb, V // P, "wo")
+
+        z_of_last_group = None
+        for g in range(N_GROUPS):
+            if g + 1 < N_GROUPS:
+                quantise_y(g + 1)
+            f_banks = transpose_first(g)
+            second = work.tile([P, PACK, GROUP], F32)
+            inter = work.tile([P, PACK, GROUP], F32)
+            relu_of_product(g, ws_codes, ws_scales, 0, second)
+            relu_of_product(g, wi_codes, wi_scales, 1, inter)
+            if g > 0:
+                output_head(g - 1, z_of_last_group[0], z_of_last_group[1])
+            z_of_last_group = gate_and_quantise(second, inter, f_banks)
+        output_head(N_GROUPS - 1, z_of_last_group[0], z_of_last_group[1])

@@ -20,6 +20,7 @@ GROUP = 512
 CHUNKS = GROUP // P
 HALF = GROUP // 2
 N_GROUPS = BATCH // GROUP
+RUN = 4
 
 FLOPS = 2 * BATCH * K * (K + K + V)
 
@@ -146,21 +147,21 @@ def tile_smcrossbaby_1_pb_t_kernel(
 
         def gate_and_quantise(second, inter, f_banks):
             z_grouped = work.tile([P, GROUP, PACK], BF16, align_bytes=64)
-            product = work.tile([P, GROUP, PACK], F32)
+            product = work.tile([P, PACK, GROUP], F32)
             for h in range(2):
                 cols = slice(h * HALF, (h + 1) * HALF)
                 nc.vector.tensor_tensor(
-                    out=product[:, cols, :].rearrange("p b (u e) -> p b u e", e=2),
-                    in0=second[:, :, cols].rearrange("p (u e) b -> p b u e", e=2),
-                    in1=f_banks[h][:].bitcast(BF16).rearrange("p u (b e) -> p b u e", e=2),
+                    out=product[:, :, cols].rearrange("p (u e) b -> p u e b", e=2),
+                    in0=second[:, :, cols].rearrange("p (u e) b -> p u e b", e=2),
+                    in1=f_banks[h][:].bitcast(BF16).rearrange("p u (b e) -> p u e b", e=2),
                     op=MULT,
                 )
             for h in range(2):
                 cols = slice(h * HALF, (h + 1) * HALF)
                 nc.vector.tensor_tensor(
-                    out=z_grouped[:, cols, :],
-                    in0=product[:, cols, :],
-                    in1=inter[:, :, cols].rearrange("p t b -> p b t"),
+                    out=z_grouped[:, cols, :].rearrange("p (c i) t -> p c t i", i=RUN),
+                    in0=product[:, :, cols].rearrange("p t (c i) -> p c t i", i=RUN),
+                    in1=inter[:, :, cols].rearrange("p t (c i) -> p c t i", i=RUN),
                     op=ADD,
                 )
             z_codes = work.tile([P, GROUP], U32, align_bytes=64)

@@ -31,7 +31,7 @@ def tile_smcrossbaby_1_pb_t_kernel(
     nc = tc.nc
     with ExitStack() as ctx:
         keep = ctx.enter_context(tc.tile_pool(name="keep", bufs=1))
-        work = ctx.enter_context(tc.tile_pool(name="work", bufs=2))
+        work = ctx.enter_context(tc.tile_pool(name="work", bufs=3))
         psum_words = ctx.enter_context(tc.psum_pool(name="psum_words", bufs=2))
         psum_acc = ctx.enter_context(tc.psum_pool(name="psum_acc", bufs=3))
         psum_out = ctx.enter_context(tc.psum_pool(name="psum_out", bufs=1))
@@ -92,7 +92,7 @@ def tile_smcrossbaby_1_pb_t_kernel(
 
         def quantise_weight(w_sb, n_chunks, name):
             cols = n_chunks * P
-            grouped = keep.tile([P, cols * PACK], BF16, align_bytes=64, name=name + "_grouped")
+            grouped = work.tile([P, cols * PACK], BF16, align_bytes=64, tag="y_grouped")
             for pair in range(n_chunks // 2):
                 bank = psum_words.tile([P, 2, 2 * P], F32, tag="y_words")
                 words_onto_partitions(bank, w_sb[:, 2 * pair, :], w_sb[:, 2 * pair + 1, :])
@@ -113,7 +113,8 @@ def tile_smcrossbaby_1_pb_t_kernel(
             for h in range(2):
                 y_words = psum_words.tile([P, 2, HALF], F32)
                 words_onto_partitions(y_words, y_sb[g][:, 2 * h, :], y_sb[g][:, 2 * h + 1, :])
-                nc.scalar.copy(
+                copy_out = nc.scalar.copy if h == 0 else nc.vector.tensor_copy
+                copy_out(
                     out=grouped_words(y_grouped, h * HALF, HALF),
                     in_=y_words[:].rearrange("p u c -> p c u"),
                 )
@@ -156,9 +157,9 @@ def tile_smcrossbaby_1_pb_t_kernel(
                     in1=f_banks[h][:].bitcast(BF16).rearrange("p u (b e) -> p u e b", e=2),
                     op=MULT,
                 )
-            for h in range(2):
-                cols = slice(h * HALF, (h + 1) * HALF)
-                nc.vector.tensor_tensor(
+            for j in range(CHUNKS):
+                cols = slice(j * P, (j + 1) * P)
+                nc.gpsimd.tensor_tensor(
                     out=z_grouped[:, cols, :].rearrange("p (c i) t -> p c t i", i=RUN),
                     in0=product[:, :, cols].rearrange("p t (c i) -> p c t i", i=RUN),
                     in1=inter[:, :, cols].rearrange("p t (c i) -> p c t i", i=RUN),

@@ -21,6 +21,7 @@ CHUNKS = GROUP // P
 HALF = GROUP // 2
 N_GROUPS = BATCH // GROUP
 RUN = 4
+Y_AHEAD = 2
 
 FLOPS = 2 * BATCH * K * (K + K + V)
 
@@ -30,11 +31,12 @@ def tile_smcrossbaby_1_pb_t_kernel(
 ):
     nc = tc.nc
     with ExitStack() as ctx:
+        ctx.enter_context(tc.manual_schedule())
         keep = ctx.enter_context(tc.tile_pool(name="keep", bufs=1))
-        work = ctx.enter_context(tc.tile_pool(name="work", bufs=3))
+        work = ctx.enter_context(tc.tile_pool(name="work", bufs=2))
         psum_words = ctx.enter_context(tc.psum_pool(name="psum_words", bufs=2))
         psum_acc = ctx.enter_context(tc.psum_pool(name="psum_acc", bufs=3))
-        psum_out = ctx.enter_context(tc.psum_pool(name="psum_out", bufs=1))
+        psum_head = ctx.enter_context(tc.psum_pool(name="psum_head", bufs=1))
 
         ident = keep.tile([P, P], F32)
         make_identity(nc, ident[:])
@@ -56,159 +58,149 @@ def tile_smcrossbaby_1_pb_t_kernel(
             out=wi_sb[:].rearrange("p (u e) k -> p u e k", e=2),
             in_=w_int.rearrange("(u p e) k -> p u e k", u=2, e=2),
         )
+        nc.sync.dma_start(out=y_sb[1][:], in_=y_rows[1])
         nc.sync.dma_start(out=f_sb[0][:], in_=f_rows[0])
         nc.sync.dma_start(out=wo_sb[:], in_=w_out.rearrange("(c p) m -> p c m", p=P))
         for g in range(1, N_GROUPS):
-            nc.sync.dma_start(out=y_sb[g][:], in_=y_rows[g])
+            if g + 1 < N_GROUPS:
+                nc.sync.dma_start(out=y_sb[g + 1][:], in_=y_rows[g + 1])
             nc.sync.dma_start(out=f_sb[g][:], in_=f_rows[g])
 
         bs_bf = keep.tile([P, PACK], BF16)
         bi_bf = keep.tile([P, PACK], BF16)
         bout_bf = keep.tile([P, V], BF16)
-        bias = keep.tile([P, 2, PACK], F32)
-        for which, (b_bf, b_dram) in enumerate(((bs_bf, b_second), (bi_bf, b_int))):
+        for b_bf, b_dram in ((bs_bf, b_second), (bi_bf, b_int)):
             nc.scalar.dma_start(
                 out=b_bf[:].rearrange("p (u e) -> p u e", e=2),
                 in_=b_dram.rearrange("(u p e) -> p u e", u=2, e=2),
             )
-            nc.vector.tensor_copy(out=bias[:, which, :], in_=b_bf[:])
         nc.scalar.dma_start(out=bout_bf[:], in_=b_out.partition_broadcast(P))
-        bout = keep.tile([P, 2, V], F32)
-        for c in range(2):
-            nc.vector.tensor_copy(out=bout[:, c, :], in_=bout_bf[:])
 
-        def words_onto_partitions(bank, chunk_a, chunk_b):
-            for c, chunk in enumerate((chunk_a, chunk_b)):
+        def words_onto_partitions(bank, rows_sb, pair):
+            for c in range(2):
                 for u in range(2):
                     nc.tensor.transpose(
                         bank[:, u, c * P : (c + 1) * P],
-                        chunk.bitcast(F32)[:, u * P : (u + 1) * P],
+                        rows_sb[:, 2 * pair + c, :].bitcast(F32)[:, u * P : (u + 1) * P],
                         ident[:],
                     )
 
-        def grouped_words(grouped, first_col, n_cols):
-            view = grouped[:].bitcast(F32).rearrange("p (c u) -> p c u", u=2)
-            return view[:, first_col : first_col + n_cols, :]
-
-        def quantise_weight(w_sb, n_chunks, name):
-            cols = n_chunks * P
-            grouped = work.tile([P, cols * PACK], BF16, align_bytes=64, tag="y_grouped")
+        def regroup(rows_sb, n_chunks, copy_out):
+            grouped = work.tile([P, n_chunks * P * PACK], BF16, align_bytes=64, tag="grouped", bufs=3)
+            grouped_words = grouped[:].bitcast(F32).rearrange("p (c u) -> p c u", u=2)
             for pair in range(n_chunks // 2):
-                bank = psum_words.tile([P, 2, 2 * P], F32, tag="y_words")
-                words_onto_partitions(bank, w_sb[:, 2 * pair, :], w_sb[:, 2 * pair + 1, :])
-                nc.vector.tensor_copy(
-                    out=grouped_words(grouped, pair * 2 * P, 2 * P),
-                    in_=bank[:].rearrange("p u c -> p c u"),
+                words = psum_words.tile([P, 2, HALF], F32)
+                words_onto_partitions(words, rows_sb, pair)
+                copy_out(
+                    out=grouped_words[:, pair * HALF : (pair + 1) * HALF, :],
+                    in_=words[:].rearrange("p u c -> p c u"),
                 )
+            return grouped
+
+        def quantise(grouped, cols, name):
             codes = keep.tile([P, cols], U32, align_bytes=64, name=name + "_codes")
             scales = keep.tile([P, cols], U8, align_bytes=64, name=name + "_scales")
             nc.vector.quantize_mx(out=codes[:].bitcast(FP8X4), scales=scales[:], in_=grouped[:])
             return codes, scales
 
-        y_codes = [keep.tile([P, GROUP], U32, align_bytes=64, name="y_codes%d" % g) for g in range(N_GROUPS)]
-        y_scales = [keep.tile([P, GROUP], U8, align_bytes=64, name="y_scales%d" % g) for g in range(N_GROUPS)]
-
-        def quantise_y(g):
-            y_grouped = work.tile([P, GROUP * PACK], BF16, align_bytes=64)
-            for h in range(2):
-                y_words = psum_words.tile([P, 2, HALF], F32)
-                words_onto_partitions(y_words, y_sb[g][:, 2 * h, :], y_sb[g][:, 2 * h + 1, :])
-                copy_out = nc.scalar.copy if h == 0 else nc.vector.tensor_copy
-                copy_out(
-                    out=grouped_words(y_grouped, h * HALF, HALF),
-                    in_=y_words[:].rearrange("p u c -> p c u"),
-                )
-            nc.vector.quantize_mx(
-                out=y_codes[g][:].bitcast(FP8X4), scales=y_scales[g][:], in_=y_grouped[:]
-            )
-
-        def transpose_first(g):
-            banks = []
-            for h in range(2):
-                f_words = psum_words.tile([P, 2, HALF], F32)
-                words_onto_partitions(f_words, f_sb[g][:, 2 * h, :], f_sb[g][:, 2 * h + 1, :])
-                banks.append(f_words)
-            return banks
-
-        def relu_of_product(g, codes, scales, which, result):
+        def relu_of_product(y_q, w_q, w_bias, result):
             for t in range(PACK):
                 acc = psum_acc.tile([P, GROUP], F32)
                 nc.tensor.matmul_mx(
                     out=acc[:],
-                    lhsT=codes[:, t * P : (t + 1) * P].bitcast(FP8X4),
-                    lhsT_scale=scales[:, t * P : (t + 1) * P],
-                    rhs=y_codes[g][:].bitcast(FP8X4),
-                    rhs_scale=y_scales[g][:],
+                    lhsT=w_q[0][:, t * P : (t + 1) * P].bitcast(FP8X4),
+                    lhsT_scale=w_q[1][:, t * P : (t + 1) * P],
+                    rhs=y_q[0][:].bitcast(FP8X4),
+                    rhs_scale=y_q[1][:],
                     start=True,
                     stop=True,
                 )
                 nc.scalar.activation(
-                    out=result[:, t, :], in_=acc[:], func=RELU, bias=bias[:, which, t : t + 1], scale=1.0
+                    out=result[:, t, :], in_=acc[:], func=RELU, bias=w_bias[:, t : t + 1], scale=1.0
                 )
 
-        def gate_and_quantise(second, inter, f_banks):
-            z_grouped = work.tile([P, GROUP, PACK], BF16, align_bytes=64)
-            product = work.tile([P, PACK, GROUP], F32)
-            for h in range(2):
-                cols = slice(h * HALF, (h + 1) * HALF)
-                nc.vector.tensor_tensor(
-                    out=product[:, :, cols].rearrange("p (u e) b -> p u e b", e=2),
-                    in0=second[:, :, cols].rearrange("p (u e) b -> p u e b", e=2),
-                    in1=f_banks[h][:].bitcast(BF16).rearrange("p u (b e) -> p u e b", e=2),
-                    op=MULT,
-                )
-            for j in range(CHUNKS):
-                cols = slice(j * P, (j + 1) * P)
-                nc.gpsimd.tensor_tensor(
-                    out=z_grouped[:, cols, :].rearrange("p (c i) t -> p c t i", i=RUN),
-                    in0=product[:, :, cols].rearrange("p t (c i) -> p c t i", i=RUN),
-                    in1=inter[:, :, cols].rearrange("p t (c i) -> p c t i", i=RUN),
-                    op=ADD,
-                )
-            z_codes = work.tile([P, GROUP], U32, align_bytes=64)
-            z_scales = work.tile([P, GROUP], U8, align_bytes=64)
-            nc.vector.quantize_mx(
-                out=z_codes[:].bitcast(FP8X4),
-                scales=z_scales[:],
-                in_=z_grouped[:].rearrange("p b t -> p (b t)"),
+        def times_first(product, second, f_words, h):
+            cols = slice(h * HALF, (h + 1) * HALF)
+            nc.vector.tensor_tensor(
+                out=product[:, :, cols].rearrange("p (u e) b -> p u e b", e=2),
+                in0=second[:, :, cols].rearrange("p (u e) b -> p u e b", e=2),
+                in1=f_words[:].bitcast(BF16).rearrange("p u (b e) -> p u e b", e=2),
+                op=MULT,
             )
-            return z_codes, z_scales
 
-        def output_head(g, z_codes, z_scales):
-            out_sb = work.tile([P, CHUNKS, V], F32)
-            for pair in range(CHUNKS // 2):
-                head = psum_out.tile([P, 2, V], F32)
-                for c in range(2):
-                    j = 2 * pair + c
-                    nc.tensor.matmul_mx(
-                        out=head[:, c, :],
-                        lhsT=z_codes[:, j * P : (j + 1) * P].bitcast(FP8X4),
-                        lhsT_scale=z_scales[:, j * P : (j + 1) * P],
-                        rhs=wo_codes[:].bitcast(FP8X4),
-                        rhs_scale=wo_scales[:],
-                        start=True,
-                        stop=True,
-                    )
-                nc.vector.tensor_tensor(
-                    out=out_sb[:, 2 * pair : 2 * pair + 2, :], in0=head[:], in1=bout[:], op=ADD
+        def output_head(g, z_q, pair):
+            head = psum_head.tile([P, 2, V], F32)
+            for c in range(2):
+                j = 2 * pair + c
+                nc.tensor.matmul_mx(
+                    out=head[:, c, :],
+                    lhsT=z_q[0][:, j * P : (j + 1) * P].bitcast(FP8X4),
+                    lhsT_scale=z_q[1][:, j * P : (j + 1) * P],
+                    rhs=wo_q[0][:].bitcast(FP8X4),
+                    rhs_scale=wo_q[1][:],
+                    start=True,
+                    stop=True,
                 )
-            nc.sync.dma_start(out=out_rows[g], in_=out_sb[:])
+            out_sb = work.tile([P, 2, V], F32, bufs=4)
+            nc.vector.tensor_tensor(out=out_sb[:], in0=head[:], in1=bout[:], op=ADD)
+            nc.sync.dma_start(out=out_rows[g][:, 2 * pair : 2 * pair + 2, :], in_=out_sb[:])
 
-        quantise_y(0)
-        ws_codes, ws_scales = quantise_weight(ws_sb, PACK, "ws")
-        wi_codes, wi_scales = quantise_weight(wi_sb, PACK, "wi")
-        wo_codes, wo_scales = quantise_weight(wo_sb, V // P, "wo")
+        y_q = [None] * N_GROUPS
+        y_grouped = regroup(y_sb[0], CHUNKS, nc.scalar.copy)
+        ws_grouped = regroup(ws_sb, PACK, nc.vector.tensor_copy)
+        wi_grouped = regroup(wi_sb, PACK, nc.scalar.copy)
+        y_q[0] = quantise(y_grouped, GROUP, "y0")
+        ws_q = quantise(ws_grouped, K, "ws")
+        bs = keep.tile([P, PACK], F32)
+        bi = keep.tile([P, PACK], F32)
+        nc.vector.tensor_copy(out=bs[:], in_=bs_bf[:])
+        nc.vector.tensor_copy(out=bi[:], in_=bi_bf[:])
+        y_grouped = regroup(y_sb[1], CHUNKS, nc.scalar.copy)
+        wi_q = quantise(wi_grouped, K, "wi")
+        wo_grouped = regroup(wo_sb, V // P, nc.vector.tensor_copy)
+        y_q[1] = quantise(y_grouped, GROUP, "y1")
+        wo_q = quantise(wo_grouped, V, "wo")
+        bout = keep.tile([P, 2, V], F32)
+        for c in range(2):
+            nc.vector.tensor_copy(out=bout[:, c, :], in_=bout_bf[:])
 
-        z_of_last_group = None
-        for g in range(N_GROUPS):
-            if g + 1 < N_GROUPS:
-                quantise_y(g + 1)
-            f_banks = transpose_first(g)
-            second = work.tile([P, PACK, GROUP], F32)
-            inter = work.tile([P, PACK, GROUP], F32)
-            relu_of_product(g, ws_codes, ws_scales, 0, second)
-            relu_of_product(g, wi_codes, wi_scales, 1, inter)
-            if g > 0:
-                output_head(g - 1, z_of_last_group[0], z_of_last_group[1])
-            z_of_last_group = gate_and_quantise(second, inter, f_banks)
-        output_head(N_GROUPS - 1, z_of_last_group[0], z_of_last_group[1])
+        z_q = None
+        for g in range(N_GROUPS + 1):
+            if g < N_GROUPS:
+                second = work.tile([P, PACK, GROUP], F32)
+                inter = work.tile([P, PACK, GROUP], F32)
+                product = work.tile([P, PACK, GROUP], F32)
+                relu_of_product(y_q[g], ws_q, bs, second)
+                f_banks = []
+                for h in range(2):
+                    f_words = psum_words.tile([P, 2, HALF], F32)
+                    words_onto_partitions(f_words, f_sb[g], h)
+                    f_banks.append(f_words)
+                if g + Y_AHEAD < N_GROUPS:
+                    y_grouped = regroup(y_sb[g + Y_AHEAD], CHUNKS, nc.scalar.copy)
+                relu_of_product(y_q[g], wi_q, bi, inter)
+            for h in range(2):
+                if g < N_GROUPS:
+                    times_first(product, second, f_banks[h], h)
+                if g > 0:
+                    output_head(g - 1, z_q, h)
+            if g + Y_AHEAD < N_GROUPS:
+                y_q[g + Y_AHEAD] = quantise(y_grouped, GROUP, "y%d" % (g + Y_AHEAD))
+            if g < N_GROUPS:
+                z_grouped = work.tile([P, GROUP, PACK], BF16, align_bytes=64)
+                for h in range(2):
+                    cols = slice(h * HALF, (h + 1) * HALF)
+                    nc.vector.tensor_tensor(
+                        out=z_grouped[:, cols, :].rearrange("p (c i) t -> p c t i", i=RUN),
+                        in0=product[:, :, cols].rearrange("p t (c i) -> p c t i", i=RUN),
+                        in1=inter[:, :, cols].rearrange("p t (c i) -> p c t i", i=RUN),
+                        op=ADD,
+                    )
+                z_codes = work.tile([P, GROUP], U32, align_bytes=64)
+                z_scales = work.tile([P, GROUP], U8, align_bytes=64)
+                nc.vector.quantize_mx(
+                    out=z_codes[:].bitcast(FP8X4),
+                    scales=z_scales[:],
+                    in_=z_grouped[:].rearrange("p b t -> p (b t)"),
+                )
+                z_q = (z_codes, z_scales)

@@ -22,6 +22,8 @@ HALF = GROUP // 2
 N_GROUPS = BATCH // GROUP
 RUN = 4
 Y_AHEAD = 2
+GATE_LAG = 1
+HEAD_LAG = 2
 
 FLOPS = 2 * BATCH * K * (K + K + V)
 
@@ -34,7 +36,7 @@ def tile_smcrossbaby_1_pb_t_kernel(
         ctx.enter_context(tc.manual_schedule())
         keep = ctx.enter_context(tc.tile_pool(name="keep", bufs=1))
         work = ctx.enter_context(tc.tile_pool(name="work", bufs=2))
-        psum_words = ctx.enter_context(tc.psum_pool(name="psum_words", bufs=2))
+        psum_words = ctx.enter_context(tc.psum_pool(name="psum_words", bufs=4))
         psum_acc = ctx.enter_context(tc.psum_pool(name="psum_acc", bufs=3))
         psum_head = ctx.enter_context(tc.psum_pool(name="psum_head", bufs=1))
 
@@ -49,48 +51,46 @@ def tile_smcrossbaby_1_pb_t_kernel(
         ws_sb = keep.tile([P, PACK, K], BF16)
         wi_sb = keep.tile([P, PACK, K], BF16)
         wo_sb = keep.tile([P, V // P, K], BF16)
-        nc.sync.dma_start(out=y_sb[0][:], in_=y_rows[0])
+        bout_bf = keep.tile([P, V], BF16)
         nc.sync.dma_start(
             out=ws_sb[:].rearrange("p (u e) k -> p u e k", e=2),
             in_=w_second.rearrange("(u p e) k -> p u e k", u=2, e=2),
         )
+        nc.sync.dma_start(out=y_sb[0][:], in_=y_rows[0])
         nc.sync.dma_start(
             out=wi_sb[:].rearrange("p (u e) k -> p u e k", e=2),
             in_=w_int.rearrange("(u p e) k -> p u e k", u=2, e=2),
         )
-        nc.sync.dma_start(out=y_sb[1][:], in_=y_rows[1])
         nc.sync.dma_start(out=f_sb[0][:], in_=f_rows[0])
+        for g in range(1, Y_AHEAD + 1):
+            nc.sync.dma_start(out=y_sb[g][:], in_=y_rows[g])
         nc.sync.dma_start(out=wo_sb[:], in_=w_out.rearrange("(c p) m -> p c m", p=P))
+        nc.sync.dma_start(out=bout_bf[:], in_=b_out.partition_broadcast(P))
         for g in range(1, N_GROUPS):
-            if g + 1 < N_GROUPS:
-                nc.sync.dma_start(out=y_sb[g + 1][:], in_=y_rows[g + 1])
             nc.sync.dma_start(out=f_sb[g][:], in_=f_rows[g])
+            if g + Y_AHEAD < N_GROUPS:
+                nc.sync.dma_start(out=y_sb[g + Y_AHEAD][:], in_=y_rows[g + Y_AHEAD])
 
         bs_bf = keep.tile([P, PACK], BF16)
         bi_bf = keep.tile([P, PACK], BF16)
-        bout_bf = keep.tile([P, V], BF16)
         for b_bf, b_dram in ((bs_bf, b_second), (bi_bf, b_int)):
             nc.scalar.dma_start(
                 out=b_bf[:].rearrange("p (u e) -> p u e", e=2),
                 in_=b_dram.rearrange("(u p e) -> p u e", u=2, e=2),
             )
-        nc.scalar.dma_start(out=bout_bf[:], in_=b_out.partition_broadcast(P))
-
-        def words_onto_partitions(bank, rows_sb, pair):
-            for c in range(2):
-                for u in range(2):
-                    nc.tensor.transpose(
-                        bank[:, u, c * P : (c + 1) * P],
-                        rows_sb[:, 2 * pair + c, :].bitcast(F32)[:, u * P : (u + 1) * P],
-                        ident[:],
-                    )
 
         def regroup(rows_sb, n_chunks, copy_out):
             grouped = work.tile([P, n_chunks * P * PACK], BF16, align_bytes=64, tag="grouped", bufs=3)
             grouped_words = grouped[:].bitcast(F32).rearrange("p (c u) -> p c u", u=2)
             for pair in range(n_chunks // 2):
-                words = psum_words.tile([P, 2, HALF], F32)
-                words_onto_partitions(words, rows_sb, pair)
+                words = psum_words.tile([P, 2, HALF], F32, tag="words")
+                for c in range(2):
+                    for u in range(2):
+                        nc.tensor.transpose(
+                            words[:, u, c * P : (c + 1) * P],
+                            rows_sb[:, 2 * pair + c, :].bitcast(F32)[:, u * P : (u + 1) * P],
+                            ident[:],
+                        )
                 copy_out(
                     out=grouped_words[:, pair * HALF : (pair + 1) * HALF, :],
                     in_=words[:].rearrange("p u c -> p c u"),
@@ -119,19 +119,48 @@ def tile_smcrossbaby_1_pb_t_kernel(
                     out=result[:, t, :], in_=acc[:], func=RELU, bias=w_bias[:, t : t + 1], scale=1.0
                 )
 
-        def times_first(product, second, f_words, h):
-            cols = slice(h * HALF, (h + 1) * HALF)
+        def first_words(rows_sb):
+            banks = []
+            for u in range(2):
+                f_words = psum_words.tile([P, GROUP], F32, tag="words")
+                for c in range(CHUNKS):
+                    nc.tensor.transpose(
+                        f_words[:, c * P : (c + 1) * P],
+                        rows_sb[:, c, :].bitcast(F32)[:, u * P : (u + 1) * P],
+                        ident[:],
+                    )
+                banks.append(f_words)
+            return banks
+
+        def times_first(product, second, f_words, u):
             nc.vector.tensor_tensor(
-                out=product[:, :, cols].rearrange("p (u e) b -> p u e b", e=2),
-                in0=second[:, :, cols].rearrange("p (u e) b -> p u e b", e=2),
-                in1=f_words[:].bitcast(BF16).rearrange("p u (b e) -> p u e b", e=2),
+                out=product[:, 2 * u : 2 * u + 2, :],
+                in0=second[:, 2 * u : 2 * u + 2, :],
+                in1=f_words[:].bitcast(BF16).rearrange("p (b e) -> p e b", e=2),
                 op=MULT,
             )
 
-        def output_head(g, z_q, pair):
+        def plus_inter(z_grouped, product, inter, h):
+            cols = slice(h * HALF, (h + 1) * HALF)
+            nc.vector.tensor_tensor(
+                out=z_grouped[:, cols, :].rearrange("p (c i) t -> p c t i", i=RUN),
+                in0=product[:, :, cols].rearrange("p t (c i) -> p c t i", i=RUN),
+                in1=inter[:, :, cols].rearrange("p t (c i) -> p c t i", i=RUN),
+                op=ADD,
+            )
+
+        def quantise_z_half(z_grouped, z_codes, z_scales, h):
+            cols = slice(h * HALF, (h + 1) * HALF)
+            nc.vector.quantize_mx(
+                out=z_codes[:, cols].bitcast(FP8X4),
+                scales=z_scales[:, cols],
+                in_=z_grouped[:, cols, :].rearrange("p b t -> p (b t)"),
+            )
+
+        def head_products(z_q, h):
             head = psum_head.tile([P, 2, V], F32)
             for c in range(2):
-                j = 2 * pair + c
+                j = 2 * h + c
                 nc.tensor.matmul_mx(
                     out=head[:, c, :],
                     lhsT=z_q[0][:, j * P : (j + 1) * P].bitcast(FP8X4),
@@ -141,66 +170,67 @@ def tile_smcrossbaby_1_pb_t_kernel(
                     start=True,
                     stop=True,
                 )
+            return head
+
+        def add_b_out_and_store(g, head, h):
             out_sb = work.tile([P, 2, V], F32, bufs=4)
-            nc.vector.tensor_tensor(out=out_sb[:], in0=head[:], in1=bout[:], op=ADD)
-            nc.sync.dma_start(out=out_rows[g][:, 2 * pair : 2 * pair + 2, :], in_=out_sb[:])
+            nc.vector.tensor_tensor(
+                out=out_sb[:], in0=head[:], in1=bout_bf[:].unsqueeze(1).to_broadcast([P, 2, V]), op=ADD
+            )
+            nc.sync.dma_start(out=out_rows[g][:, 2 * h : 2 * h + 2, :], in_=out_sb[:])
 
-        y_q = [None] * N_GROUPS
-        y_grouped = regroup(y_sb[0], CHUNKS, nc.scalar.copy)
         ws_grouped = regroup(ws_sb, PACK, nc.vector.tensor_copy)
-        wi_grouped = regroup(wi_sb, PACK, nc.scalar.copy)
-        y_q[0] = quantise(y_grouped, GROUP, "y0")
+        y_grouped = {0: regroup(y_sb[0], CHUNKS, nc.scalar.copy)}
         ws_q = quantise(ws_grouped, K, "ws")
-        bs = keep.tile([P, PACK], F32)
-        bi = keep.tile([P, PACK], F32)
-        nc.vector.tensor_copy(out=bs[:], in_=bs_bf[:])
-        nc.vector.tensor_copy(out=bi[:], in_=bi_bf[:])
-        y_grouped = regroup(y_sb[1], CHUNKS, nc.scalar.copy)
+        y_q = {0: quantise(y_grouped[0], GROUP, "y0")}
+        wi_grouped = regroup(wi_sb, PACK, nc.scalar.copy)
         wi_q = quantise(wi_grouped, K, "wi")
-        wo_grouped = regroup(wo_sb, V // P, nc.vector.tensor_copy)
-        y_q[1] = quantise(y_grouped, GROUP, "y1")
-        wo_q = quantise(wo_grouped, V, "wo")
-        bout = keep.tile([P, 2, V], F32)
-        for c in range(2):
-            nc.vector.tensor_copy(out=bout[:, c, :], in_=bout_bf[:])
 
-        z_q = None
-        for g in range(N_GROUPS + 1):
-            if g < N_GROUPS:
-                second = work.tile([P, PACK, GROUP], F32)
-                inter = work.tile([P, PACK, GROUP], F32)
+        def quantise_next_y():
+            g = len(y_q)
+            if g < len(y_grouped):
+                y_q[g] = quantise(y_grouped[g], GROUP, "y%d" % g)
+
+        stage1 = {}
+        z_q = {}
+        for r in range(N_GROUPS + HEAD_LAG):
+            in_stage1, in_gate, in_head = r < N_GROUPS, 0 <= r - GATE_LAG < N_GROUPS, 0 <= r - HEAD_LAG
+            if in_head:
+                head = head_products(z_q[r - HEAD_LAG], 0)
+            if in_gate:
+                second, inter, f_banks = stage1[r - GATE_LAG]
                 product = work.tile([P, PACK, GROUP], F32)
-                relu_of_product(y_q[g], ws_q, bs, second)
-                f_banks = []
-                for h in range(2):
-                    f_words = psum_words.tile([P, 2, HALF], F32)
-                    words_onto_partitions(f_words, f_sb[g], h)
-                    f_banks.append(f_words)
-                if g + Y_AHEAD < N_GROUPS:
-                    y_grouped = regroup(y_sb[g + Y_AHEAD], CHUNKS, nc.scalar.copy)
-                relu_of_product(y_q[g], wi_q, bi, inter)
-            for h in range(2):
-                if g < N_GROUPS:
-                    times_first(product, second, f_banks[h], h)
-                if g > 0:
-                    output_head(g - 1, z_q, h)
-            if g + Y_AHEAD < N_GROUPS:
-                y_q[g + Y_AHEAD] = quantise(y_grouped, GROUP, "y%d" % (g + Y_AHEAD))
-            if g < N_GROUPS:
+                for u in range(2):
+                    times_first(product, second, f_banks[u], u)
+            if in_head:
+                add_b_out_and_store(r - HEAD_LAG, head, 0)
+            if in_gate:
                 z_grouped = work.tile([P, GROUP, PACK], BF16, align_bytes=64)
-                for h in range(2):
-                    cols = slice(h * HALF, (h + 1) * HALF)
-                    nc.vector.tensor_tensor(
-                        out=z_grouped[:, cols, :].rearrange("p (c i) t -> p c t i", i=RUN),
-                        in0=product[:, :, cols].rearrange("p t (c i) -> p c t i", i=RUN),
-                        in1=inter[:, :, cols].rearrange("p t (c i) -> p c t i", i=RUN),
-                        op=ADD,
-                    )
+                plus_inter(z_grouped, product, inter, 0)
+            quantise_next_y()
+            if in_gate:
+                plus_inter(z_grouped, product, inter, 1)
+            quantise_next_y()
+            if r == HEAD_LAG - 1:
+                wo_q = quantise(regroup(wo_sb, V // P, nc.vector.tensor_copy), V, "wo")
+            if in_stage1:
+                new_second = work.tile([P, PACK, GROUP], F32)
+                new_inter = work.tile([P, PACK, GROUP], F32)
+                relu_of_product(y_q[r], ws_q, bs_bf, new_second)
+                new_f_banks = first_words(f_sb[r])
+            if in_head:
+                head = head_products(z_q[r - HEAD_LAG], 1)
+            if in_stage1:
+                relu_of_product(y_q[r], wi_q, bi_bf, new_inter)
+                stage1[r] = (new_second, new_inter, new_f_banks)
+                for g in range(len(y_grouped), min(r + Y_AHEAD, N_GROUPS - 1) + 1):
+                    y_grouped[g] = regroup(y_sb[g], CHUNKS, nc.scalar.copy)
+            if in_gate:
                 z_codes = work.tile([P, GROUP], U32, align_bytes=64)
                 z_scales = work.tile([P, GROUP], U8, align_bytes=64)
-                nc.vector.quantize_mx(
-                    out=z_codes[:].bitcast(FP8X4),
-                    scales=z_scales[:],
-                    in_=z_grouped[:].rearrange("p b t -> p (b t)"),
-                )
-                z_q = (z_codes, z_scales)
+                z_q[r - GATE_LAG] = (z_codes, z_scales)
+                quantise_z_half(z_grouped, z_codes, z_scales, 0)
+            if in_head:
+                add_b_out_and_store(r - HEAD_LAG, head, 1)
+            if in_gate:
+                quantise_z_half(z_grouped, z_codes, z_scales, 1)

@@ -132,17 +132,19 @@ def tile_smcrossbaby_1_pb_t_kernel(
                 banks.append(f_words)
             return banks
 
-        def times_first(product, second, f_words, u):
-            nc.vector.tensor_tensor(
-                out=product[:, 2 * u : 2 * u + 2, :],
-                in0=second[:, 2 * u : 2 * u + 2, :],
-                in1=f_words[:].bitcast(BF16).rearrange("p (b e) -> p e b", e=2),
-                op=MULT,
-            )
-
-        def plus_inter(z_grouped, product, inter, h):
+        def times_first(product, second, f_banks, h):
             cols = slice(h * HALF, (h + 1) * HALF)
-            nc.vector.tensor_tensor(
+            for u in range(2):
+                nc.vector.tensor_tensor(
+                    out=product[:, 2 * u : 2 * u + 2, cols],
+                    in0=second[:, 2 * u : 2 * u + 2, cols],
+                    in1=f_banks[u][:].bitcast(BF16).rearrange("p (b e) -> p e b", e=2)[:, :, cols],
+                    op=MULT,
+                )
+
+        def plus_inter(engine, z_grouped, product, inter, h):
+            cols = slice(h * HALF, (h + 1) * HALF)
+            engine.tensor_tensor(
                 out=z_grouped[:, cols, :].rearrange("p (c i) t -> p c t i", i=RUN),
                 in0=product[:, :, cols].rearrange("p t (c i) -> p c t i", i=RUN),
                 in1=inter[:, :, cols].rearrange("p t (c i) -> p c t i", i=RUN),
@@ -200,17 +202,15 @@ def tile_smcrossbaby_1_pb_t_kernel(
             if in_gate:
                 second, inter, f_banks = stage1[r - GATE_LAG]
                 product = work.tile([P, PACK, GROUP], F32)
-                for u in range(2):
-                    times_first(product, second, f_banks[u], u)
+                z_grouped = work.tile([P, GROUP, PACK], BF16, align_bytes=64)
+                times_first(product, second, f_banks, 1)
+                plus_inter(nc.gpsimd, z_grouped, product, inter, 1)
             if in_head:
                 add_b_out_and_store(r - HEAD_LAG, head, 0)
             if in_gate:
-                z_grouped = work.tile([P, GROUP, PACK], BF16, align_bytes=64)
-                plus_inter(z_grouped, product, inter, 0)
-            quantise_next_y()
-            if in_gate:
-                plus_inter(z_grouped, product, inter, 1)
-            quantise_next_y()
+                times_first(product, second, f_banks, 0)
+            if r not in y_q:
+                quantise_next_y()
             if r == HEAD_LAG - 1:
                 wo_q = quantise(regroup(wo_sb, V // P, nc.vector.tensor_copy), V, "wo")
             if in_stage1:
@@ -220,6 +220,10 @@ def tile_smcrossbaby_1_pb_t_kernel(
                 new_f_banks = first_words(f_sb[r])
             if in_head:
                 head = head_products(z_q[r - HEAD_LAG], 1)
+                add_b_out_and_store(r - HEAD_LAG, head, 1)
+            if in_gate:
+                plus_inter(nc.vector, z_grouped, product, inter, 0)
+            quantise_next_y()
             if in_stage1:
                 relu_of_product(y_q[r], wi_q, bi_bf, new_inter)
                 stage1[r] = (new_second, new_inter, new_f_banks)
@@ -229,8 +233,5 @@ def tile_smcrossbaby_1_pb_t_kernel(
                 z_codes = work.tile([P, GROUP], U32, align_bytes=64)
                 z_scales = work.tile([P, GROUP], U8, align_bytes=64)
                 z_q[r - GATE_LAG] = (z_codes, z_scales)
-                quantise_z_half(z_grouped, z_codes, z_scales, 0)
-            if in_head:
-                add_b_out_and_store(r - HEAD_LAG, head, 1)
-            if in_gate:
                 quantise_z_half(z_grouped, z_codes, z_scales, 1)
+                quantise_z_half(z_grouped, z_codes, z_scales, 0)

@@ -16,12 +16,11 @@ P = 128
 PACK = 4
 K = P * PACK
 BATCH, V = 4096, 256
-GROUP = 512
-CHUNKS = GROUP // P
-HALF = GROUP // 2
-N_GROUPS = BATCH // GROUP
+SIZES = (256, 512, 512, 512, 512, 512, 512, 512, 256)
+N_GROUPS = len(SIZES)
+STARTS = tuple(sum(SIZES[:g]) for g in range(N_GROUPS))
+BANK = 512
 RUN = 4
-Y_AHEAD = 2
 GATE_LAG = 1
 HEAD_LAG = 2
 
@@ -43,33 +42,42 @@ def tile_smcrossbaby_1_pb_t_kernel(
         ident = keep.tile([P, P], F32)
         make_identity(nc, ident[:])
 
-        y_rows = y2.rearrange("(g p j) k -> g p j k", p=P, j=CHUNKS)
-        f_rows = first.rearrange("(g p j) m -> g p j m", p=P, j=CHUNKS)
-        out_rows = out.rearrange("(g p j) v -> g p j v", p=P, j=CHUNKS)
-        y_sb = [keep.tile([P, CHUNKS, K], BF16, name="y_sb%d" % g) for g in range(N_GROUPS)]
-        f_sb = [keep.tile([P, CHUNKS, K], BF16, name="f_sb%d" % g) for g in range(N_GROUPS)]
-        ws_sb = keep.tile([P, PACK, K], BF16)
-        wi_sb = keep.tile([P, PACK, K], BF16)
+        def group_rows(dram, g):
+            return dram[STARTS[g] : STARTS[g] + SIZES[g], :].rearrange("(p j) k -> p j k", j=SIZES[g] // P)
+
+        y_sb = [keep.tile([P, SIZES[g] // P, K], BF16, name="y_sb%d" % g) for g in range(N_GROUPS)]
+        f_sb = [keep.tile([P, SIZES[g] // P, K], BF16, name="f_sb%d" % g) for g in range(N_GROUPS)]
+        ws_sb = [keep.tile([P, 2, K], BF16, name="ws_sb%d" % u) for u in range(2)]
+        wi_sb = [keep.tile([P, 2, K], BF16, name="wi_sb%d" % u) for u in range(2)]
         wo_sb = keep.tile([P, V // P, K], BF16)
         bout_bf = keep.tile([P, V], BF16)
-        nc.sync.dma_start(
-            out=ws_sb[:].rearrange("p (u e) k -> p u e k", e=2),
-            in_=w_second.rearrange("(u p e) k -> p u e k", u=2, e=2),
-        )
-        nc.sync.dma_start(out=y_sb[0][:], in_=y_rows[0])
-        nc.sync.dma_start(
-            out=wi_sb[:].rearrange("p (u e) k -> p u e k", e=2),
-            in_=w_int.rearrange("(u p e) k -> p u e k", u=2, e=2),
-        )
-        nc.sync.dma_start(out=f_sb[0][:], in_=f_rows[0])
-        for g in range(1, Y_AHEAD + 1):
-            nc.sync.dma_start(out=y_sb[g][:], in_=y_rows[g])
+
+        def load_weight(w_sb, w, u):
+            nc.sync.dma_start(
+                out=w_sb[u][:], in_=w[256 * u : 256 * u + 256, :].rearrange("(p e) k -> p e k", e=2)
+            )
+
+        def load_y(g):
+            nc.sync.dma_start(out=y_sb[g][:], in_=group_rows(y2, g))
+
+        def load_f(g):
+            nc.sync.dma_start(out=f_sb[g][:], in_=group_rows(first, g))
+
+        load_y(0)
+        load_weight(ws_sb, w_second, 0)
+        load_weight(ws_sb, w_second, 1)
+        load_weight(wi_sb, w_int, 0)
+        load_weight(wi_sb, w_int, 1)
+        load_f(0)
+        load_y(1)
+        load_f(1)
+        load_y(2)
         nc.sync.dma_start(out=wo_sb[:], in_=w_out.rearrange("(c p) m -> p c m", p=P))
         nc.sync.dma_start(out=bout_bf[:], in_=b_out.partition_broadcast(P))
-        for g in range(1, N_GROUPS):
-            nc.sync.dma_start(out=f_sb[g][:], in_=f_rows[g])
-            if g + Y_AHEAD < N_GROUPS:
-                nc.sync.dma_start(out=y_sb[g + Y_AHEAD][:], in_=y_rows[g + Y_AHEAD])
+        for g in range(2, N_GROUPS):
+            load_f(g)
+            if g + 1 < N_GROUPS:
+                load_y(g + 1)
 
         bs_bf = keep.tile([P, PACK], BF16)
         bi_bf = keep.tile([P, PACK], BF16)
@@ -79,39 +87,46 @@ def tile_smcrossbaby_1_pb_t_kernel(
                 in_=b_dram.rearrange("(u p e) -> p u e", u=2, e=2),
             )
 
-        def regroup(rows_sb, n_chunks, copy_out):
-            grouped = work.tile([P, n_chunks * P * PACK], BF16, align_bytes=64, tag="grouped", bufs=3)
+        def regroup_pair(grouped, pair, rows_sb, chunk, copy_out):
+            words = psum_words.tile([P, 2, 2 * P], F32, tag="words")
+            for c in range(2):
+                for u in range(2):
+                    nc.tensor.transpose(
+                        words[:, u, c * P : (c + 1) * P],
+                        rows_sb[:, chunk + c, :].bitcast(F32)[:, u * P : (u + 1) * P],
+                        ident[:],
+                    )
             grouped_words = grouped[:].bitcast(F32).rearrange("p (c u) -> p c u", u=2)
-            for pair in range(n_chunks // 2):
-                words = psum_words.tile([P, 2, HALF], F32, tag="words")
-                for c in range(2):
-                    for u in range(2):
-                        nc.tensor.transpose(
-                            words[:, u, c * P : (c + 1) * P],
-                            rows_sb[:, 2 * pair + c, :].bitcast(F32)[:, u * P : (u + 1) * P],
-                            ident[:],
-                        )
-                copy_out(
-                    out=grouped_words[:, pair * HALF : (pair + 1) * HALF, :],
-                    in_=words[:].rearrange("p u c -> p c u"),
-                )
+            copy_out(
+                out=grouped_words[:, pair * 2 * P : (pair + 1) * 2 * P, :],
+                in_=words[:].rearrange("p u c -> p c u"),
+            )
+
+        def new_grouped(rows):
+            grouped = work.tile([P, rows * PACK], BF16, align_bytes=64, tag="grouped", bufs=3)
             return grouped
 
-        def quantise(grouped, cols, name):
+        def new_quantised(cols, name):
             codes = keep.tile([P, cols], U32, align_bytes=64, name=name + "_codes")
             scales = keep.tile([P, cols], U8, align_bytes=64, name=name + "_scales")
-            nc.vector.quantize_mx(out=codes[:].bitcast(FP8X4), scales=scales[:], in_=grouped[:])
             return codes, scales
 
-        def relu_of_product(y_q, w_q, w_bias, result):
-            for t in range(PACK):
-                acc = psum_acc.tile([P, GROUP], F32)
+        def quantise(q, grouped, start, cols):
+            nc.vector.quantize_mx(
+                out=q[0][:, start : start + cols].bitcast(FP8X4),
+                scales=q[1][:, start : start + cols],
+                in_=grouped[:, PACK * start : PACK * (start + cols)],
+            )
+
+        def relu_of_product(g, w_q, w_bias, result, ts):
+            for t in ts:
+                acc = psum_acc.tile([P, SIZES[g]], F32, tag="acc")
                 nc.tensor.matmul_mx(
                     out=acc[:],
                     lhsT=w_q[0][:, t * P : (t + 1) * P].bitcast(FP8X4),
                     lhsT_scale=w_q[1][:, t * P : (t + 1) * P],
-                    rhs=y_q[0][:].bitcast(FP8X4),
-                    rhs_scale=y_q[1][:],
+                    rhs=y_q[g][0][:].bitcast(FP8X4),
+                    rhs_scale=y_q[g][1][:],
                     start=True,
                     stop=True,
                 )
@@ -119,21 +134,25 @@ def tile_smcrossbaby_1_pb_t_kernel(
                     out=result[:, t, :], in_=acc[:], func=RELU, bias=w_bias[:, t : t + 1], scale=1.0
                 )
 
-        def first_words(rows_sb):
+        def first_words(g):
             banks = []
             for u in range(2):
-                f_words = psum_words.tile([P, GROUP], F32, tag="words")
-                for c in range(CHUNKS):
+                f_words = psum_words.tile([P, SIZES[g]], F32, tag="words")
+                for c in range(SIZES[g] // P):
                     nc.tensor.transpose(
                         f_words[:, c * P : (c + 1) * P],
-                        rows_sb[:, c, :].bitcast(F32)[:, u * P : (u + 1) * P],
+                        f_sb[g][:, c, :].bitcast(F32)[:, u * P : (u + 1) * P],
                         ident[:],
                     )
                 banks.append(f_words)
             return banks
 
-        def times_first(product, second, f_banks, h):
-            cols = slice(h * HALF, (h + 1) * HALF)
+        def half_columns(g, h):
+            half = SIZES[g] // 2
+            return slice(h * half, (h + 1) * half)
+
+        def times_first(g, product, second, f_banks, h):
+            cols = half_columns(g, h)
             for u in range(2):
                 nc.vector.tensor_tensor(
                     out=product[:, 2 * u : 2 * u + 2, cols],
@@ -142,8 +161,8 @@ def tile_smcrossbaby_1_pb_t_kernel(
                     op=MULT,
                 )
 
-        def plus_inter(engine, z_grouped, product, inter, h):
-            cols = slice(h * HALF, (h + 1) * HALF)
+        def plus_inter(engine, g, z_grouped, product, inter, h):
+            cols = half_columns(g, h)
             engine.tensor_tensor(
                 out=z_grouped[:, cols, :].rearrange("p (c i) t -> p c t i", i=RUN),
                 in0=product[:, :, cols].rearrange("p t (c i) -> p c t i", i=RUN),
@@ -151,22 +170,23 @@ def tile_smcrossbaby_1_pb_t_kernel(
                 op=ADD,
             )
 
-        def quantise_z_half(z_grouped, z_codes, z_scales, h):
-            cols = slice(h * HALF, (h + 1) * HALF)
+        def quantise_z_half(g, z_grouped, h):
+            cols = half_columns(g, h)
             nc.vector.quantize_mx(
-                out=z_codes[:, cols].bitcast(FP8X4),
-                scales=z_scales[:, cols],
+                out=z_q[g][0][:, cols].bitcast(FP8X4),
+                scales=z_q[g][1][:, cols],
                 in_=z_grouped[:, cols, :].rearrange("p b t -> p (b t)"),
             )
 
-        def head_products(z_q, h):
-            head = psum_head.tile([P, 2, V], F32)
-            for c in range(2):
-                j = 2 * h + c
+        def head_products(g, h):
+            chunks = SIZES[g] // P // 2
+            head = psum_head.tile([P, chunks, V], F32, tag="head")
+            for c in range(chunks):
+                j = chunks * h + c
                 nc.tensor.matmul_mx(
                     out=head[:, c, :],
-                    lhsT=z_q[0][:, j * P : (j + 1) * P].bitcast(FP8X4),
-                    lhsT_scale=z_q[1][:, j * P : (j + 1) * P],
+                    lhsT=z_q[g][0][:, j * P : (j + 1) * P].bitcast(FP8X4),
+                    lhsT_scale=z_q[g][1][:, j * P : (j + 1) * P],
                     rhs=wo_q[0][:].bitcast(FP8X4),
                     rhs_scale=wo_q[1][:],
                     start=True,
@@ -175,63 +195,89 @@ def tile_smcrossbaby_1_pb_t_kernel(
             return head
 
         def add_b_out_and_store(g, head, h):
-            out_sb = work.tile([P, 2, V], F32, bufs=4)
+            chunks = SIZES[g] // P // 2
+            out_sb = work.tile([P, chunks, V], F32, bufs=4, tag="out")
             nc.vector.tensor_tensor(
-                out=out_sb[:], in0=head[:], in1=bout_bf[:].unsqueeze(1).to_broadcast([P, 2, V]), op=ADD
+                out=out_sb[:], in0=head[:], in1=bout_bf[:].unsqueeze(1).to_broadcast([P, chunks, V]), op=ADD
             )
-            nc.sync.dma_start(out=out_rows[g][:, 2 * h : 2 * h + 2, :], in_=out_sb[:])
+            nc.sync.dma_start(out=group_rows(out, g)[:, chunks * h : chunks * (h + 1), :], in_=out_sb[:])
 
-        ws_grouped = regroup(ws_sb, PACK, nc.vector.tensor_copy)
-        y_grouped = {0: regroup(y_sb[0], CHUNKS, nc.scalar.copy)}
-        ws_q = quantise(ws_grouped, K, "ws")
-        y_q = {0: quantise(y_grouped[0], GROUP, "y0")}
-        wi_grouped = regroup(wi_sb, PACK, nc.scalar.copy)
-        wi_q = quantise(wi_grouped, K, "wi")
+        y_grouped, y_q = {}, {}
 
-        def quantise_next_y():
-            g = len(y_q)
-            if g < len(y_grouped):
-                y_q[g] = quantise(y_grouped[g], GROUP, "y%d" % g)
+        def regroup_y(g, copies):
+            y_grouped[g] = new_grouped(SIZES[g])
+            for pair in range(SIZES[g] // (2 * P)):
+                regroup_pair(y_grouped[g], pair, y_sb[g], 2 * pair, copies[pair])
+
+        def quantise_y(g):
+            y_q[g] = new_quantised(SIZES[g], "y%d" % g)
+            quantise(y_q[g], y_grouped[g], 0, SIZES[g])
+
+        ws_grouped, ws_q = new_grouped(K), new_quantised(K, "ws")
+        wi_grouped = keep.tile([P, K * PACK], BF16, align_bytes=64)
+        wi_q = new_quantised(K, "wi")
+        regroup_y(0, [nc.vector.tensor_copy])
+        regroup_pair(ws_grouped, 0, ws_sb[0], 0, nc.scalar.copy)
+        quantise_y(0)
+        regroup_pair(ws_grouped, 1, ws_sb[1], 0, nc.vector.tensor_copy)
+        quantise(ws_q, ws_grouped, 0, 2 * P)
+        regroup_pair(wi_grouped, 0, wi_sb[0], 0, nc.scalar.copy)
+        quantise(ws_q, ws_grouped, 2 * P, 2 * P)
+        regroup_pair(wi_grouped, 1, wi_sb[1], 0, nc.vector.tensor_copy)
+        quantise(wi_q, wi_grouped, 0, 2 * P)
+        quantise(wi_q, wi_grouped, 2 * P, 2 * P)
 
         stage1 = {}
         z_q = {}
+        LAST = N_GROUPS - 1
         for r in range(N_GROUPS + HEAD_LAG):
-            in_stage1, in_gate, in_head = r < N_GROUPS, 0 <= r - GATE_LAG < N_GROUPS, 0 <= r - HEAD_LAG
-            if in_head:
-                head = head_products(z_q[r - HEAD_LAG], 0)
+            gate, ahead = r - GATE_LAG, r - HEAD_LAG
+            in_stage1, in_gate, in_head = r < N_GROUPS, 0 <= gate < N_GROUPS, 0 <= ahead
+            if in_stage1:
+                new_second = work.tile([P, PACK, SIZES[r]], F32, tag="second")
+                new_inter = work.tile([P, PACK, SIZES[r]], F32, tag="inter")
+                relu_of_product(r, ws_q, bs_bf, new_second, (0, 1))
             if in_gate:
-                second, inter, f_banks = stage1[r - GATE_LAG]
-                product = work.tile([P, PACK, GROUP], F32)
-                z_grouped = work.tile([P, GROUP, PACK], BF16, align_bytes=64)
-                times_first(product, second, f_banks, 1)
-                plus_inter(nc.gpsimd, z_grouped, product, inter, 1)
+                second, inter, f_banks = stage1[gate]
+                product = work.tile([P, PACK, SIZES[gate]], F32, tag="product")
+                z_grouped = work.tile([P, SIZES[gate], PACK], BF16, align_bytes=64, tag="z")
+                times_first(gate, product, second, f_banks, 1)
+                if gate < LAST:
+                    plus_inter(nc.gpsimd, gate, z_grouped, product, inter, 1)
             if in_head:
-                add_b_out_and_store(r - HEAD_LAG, head, 0)
+                head = head_products(ahead, 0)
+                add_b_out_and_store(ahead, head, 0)
+            if in_stage1:
+                relu_of_product(r, ws_q, bs_bf, new_second, (2, 3))
             if in_gate:
-                times_first(product, second, f_banks, 0)
-            if r not in y_q:
-                quantise_next_y()
+                times_first(gate, product, second, f_banks, 0)
+            if in_head:
+                head = head_products(ahead, 1)
+                add_b_out_and_store(ahead, head, 1)
+            if r == 0:
+                new_f_banks = first_words(r)
+                regroup_y(1, [nc.vector.tensor_copy, nc.vector.tensor_copy])
             if r == HEAD_LAG - 1:
-                wo_q = quantise(regroup(wo_sb, V // P, nc.vector.tensor_copy), V, "wo")
-            if in_stage1:
-                new_second = work.tile([P, PACK, GROUP], F32)
-                new_inter = work.tile([P, PACK, GROUP], F32)
-                relu_of_product(y_q[r], ws_q, bs_bf, new_second)
-                new_f_banks = first_words(f_sb[r])
-            if in_head:
-                head = head_products(z_q[r - HEAD_LAG], 1)
-                add_b_out_and_store(r - HEAD_LAG, head, 1)
+                wo_grouped, wo_q = new_grouped(V), new_quantised(V, "wo")
+                regroup_pair(wo_grouped, 0, wo_sb, 0, nc.vector.tensor_copy)
             if in_gate:
-                plus_inter(nc.vector, z_grouped, product, inter, 0)
-            quantise_next_y()
+                if gate == LAST:
+                    plus_inter(nc.vector, gate, z_grouped, product, inter, 1)
+                plus_inter(nc.vector, gate, z_grouped, product, inter, 0)
+            if r + 1 < N_GROUPS:
+                quantise_y(r + 1)
+            if r == HEAD_LAG - 1:
+                quantise(wo_q, wo_grouped, 0, V)
             if in_stage1:
-                relu_of_product(y_q[r], wi_q, bi_bf, new_inter)
+                relu_of_product(r, wi_q, bi_bf, new_inter, range(PACK))
+                if r + 2 < N_GROUPS:
+                    regroup_y(r + 2, [nc.scalar.copy, nc.scalar.copy])
+                if r > 0:
+                    new_f_banks = first_words(r)
                 stage1[r] = (new_second, new_inter, new_f_banks)
-                for g in range(len(y_grouped), min(r + Y_AHEAD, N_GROUPS - 1) + 1):
-                    y_grouped[g] = regroup(y_sb[g], CHUNKS, nc.scalar.copy)
             if in_gate:
-                z_codes = work.tile([P, GROUP], U32, align_bytes=64)
-                z_scales = work.tile([P, GROUP], U8, align_bytes=64)
-                z_q[r - GATE_LAG] = (z_codes, z_scales)
-                quantise_z_half(z_grouped, z_codes, z_scales, 1)
-                quantise_z_half(z_grouped, z_codes, z_scales, 0)
+                z_codes = work.tile([P, SIZES[gate]], U32, align_bytes=64)
+                z_scales = work.tile([P, SIZES[gate]], U8, align_bytes=64)
+                z_q[gate] = (z_codes, z_scales)
+                quantise_z_half(gate, z_grouped, 1)
+                quantise_z_half(gate, z_grouped, 0)

@@ -20,6 +20,7 @@ SIZES = (256, 512, 512, 512, 512, 512, 512, 512, 256)
 N_GROUPS = len(SIZES)
 STARTS = tuple(sum(SIZES[:g]) for g in range(N_GROUPS))
 BANK = 512
+GPSIMD_COLS = {512: 192, 256: 96}
 RUN = 4
 GATE_LAG = 1
 HEAD_LAG = 2
@@ -68,11 +69,11 @@ def tile_smcrossbaby_1_pb_t_kernel(
         load_weight(ws_sb, w_second, 1)
         load_weight(wi_sb, w_int, 0)
         load_weight(wi_sb, w_int, 1)
-        load_f(0)
         load_y(1)
-        load_f(1)
+        load_f(0)
         load_y(2)
         nc.sync.dma_start(out=wo_sb[:], in_=w_out.rearrange("(c p) m -> p c m", p=P))
+        load_f(1)
         nc.sync.dma_start(out=bout_bf[:], in_=b_out.partition_broadcast(P))
         for g in range(2, N_GROUPS):
             load_f(g)
@@ -147,12 +148,12 @@ def tile_smcrossbaby_1_pb_t_kernel(
                 banks.append(f_words)
             return banks
 
-        def half_columns(g, h):
-            half = SIZES[g] // 2
-            return slice(h * half, (h + 1) * half)
+        def part_columns(g, h):
+            cut = SIZES[g] - GPSIMD_COLS[SIZES[g]]
+            return slice(0, cut) if h == 0 else slice(cut, SIZES[g])
 
         def times_first(g, product, second, f_banks, h):
-            cols = half_columns(g, h)
+            cols = part_columns(g, h)
             for u in range(2):
                 nc.vector.tensor_tensor(
                     out=product[:, 2 * u : 2 * u + 2, cols],
@@ -162,7 +163,7 @@ def tile_smcrossbaby_1_pb_t_kernel(
                 )
 
         def plus_inter(engine, g, z_grouped, product, inter, h):
-            cols = half_columns(g, h)
+            cols = part_columns(g, h)
             engine.tensor_tensor(
                 out=z_grouped[:, cols, :].rearrange("p (c i) t -> p c t i", i=RUN),
                 in0=product[:, :, cols].rearrange("p t (c i) -> p c t i", i=RUN),
@@ -170,12 +171,11 @@ def tile_smcrossbaby_1_pb_t_kernel(
                 op=ADD,
             )
 
-        def quantise_z_half(g, z_grouped, h):
-            cols = half_columns(g, h)
+        def quantise_z(g, z_grouped, start, cols):
             nc.vector.quantize_mx(
-                out=z_q[g][0][:, cols].bitcast(FP8X4),
-                scales=z_q[g][1][:, cols],
-                in_=z_grouped[:, cols, :].rearrange("p b t -> p (b t)"),
+                out=z_q[g][0][:, start : start + cols].bitcast(FP8X4),
+                scales=z_q[g][1][:, start : start + cols],
+                in_=z_grouped[:, start : start + cols, :].rearrange("p b t -> p (b t)"),
             )
 
         def head_products(g, h):
@@ -242,36 +242,33 @@ def tile_smcrossbaby_1_pb_t_kernel(
                 product = work.tile([P, PACK, SIZES[gate]], F32, tag="product")
                 z_grouped = work.tile([P, SIZES[gate], PACK], BF16, align_bytes=64, tag="z")
                 times_first(gate, product, second, f_banks, 1)
-                if gate < LAST:
-                    plus_inter(nc.gpsimd, gate, z_grouped, product, inter, 1)
+                plus_inter(nc.gpsimd, gate, z_grouped, product, inter, 1)
             if in_head:
                 head = head_products(ahead, 0)
                 add_b_out_and_store(ahead, head, 0)
             if in_stage1:
                 relu_of_product(r, ws_q, bs_bf, new_second, (2, 3))
+            if r == 0:
+                regroup_y(1, [nc.scalar.copy, nc.vector.tensor_copy])
+                quantise_y(1)
             if in_gate:
                 times_first(gate, product, second, f_banks, 0)
             if in_head:
                 head = head_products(ahead, 1)
                 add_b_out_and_store(ahead, head, 1)
-            if r == 0:
-                new_f_banks = first_words(r)
-                regroup_y(1, [nc.vector.tensor_copy, nc.vector.tensor_copy])
-            if r == HEAD_LAG - 1:
-                wo_grouped, wo_q = new_grouped(V), new_quantised(V, "wo")
-                regroup_pair(wo_grouped, 0, wo_sb, 0, nc.vector.tensor_copy)
             if in_gate:
-                if gate == LAST:
-                    plus_inter(nc.vector, gate, z_grouped, product, inter, 1)
                 plus_inter(nc.vector, gate, z_grouped, product, inter, 0)
-            if r + 1 < N_GROUPS:
+            if 1 < r + 1 < N_GROUPS:
                 quantise_y(r + 1)
-            if r == HEAD_LAG - 1:
-                quantise(wo_q, wo_grouped, 0, V)
             if in_stage1:
                 relu_of_product(r, wi_q, bi_bf, new_inter, range(PACK))
+                if r == 0:
+                    new_f_banks = first_words(r)
                 if r + 2 < N_GROUPS:
-                    regroup_y(r + 2, [nc.scalar.copy, nc.scalar.copy])
+                    regroup_y(r + 2, [nc.vector.tensor_copy if r == 0 else nc.scalar.copy, nc.scalar.copy])
+                if r == 0:
+                    wo_grouped, wo_q = new_grouped(V), new_quantised(V, "wo")
+                    regroup_pair(wo_grouped, 0, wo_sb, 0, nc.vector.tensor_copy)
                 if r > 0:
                     new_f_banks = first_words(r)
                 stage1[r] = (new_second, new_inter, new_f_banks)
@@ -279,5 +276,6 @@ def tile_smcrossbaby_1_pb_t_kernel(
                 z_codes = work.tile([P, SIZES[gate]], U32, align_bytes=64)
                 z_scales = work.tile([P, SIZES[gate]], U8, align_bytes=64)
                 z_q[gate] = (z_codes, z_scales)
-                quantise_z_half(gate, z_grouped, 1)
-                quantise_z_half(gate, z_grouped, 0)
+                quantise_z(gate, z_grouped, 0, SIZES[gate])
+            if r == 1:
+                quantise(wo_q, wo_grouped, 0, V)

@@ -51,7 +51,15 @@ def tile_smcrossbaby_1_pb_t_kernel(
         ws_sb = [keep.tile([P, 2, K], BF16, name="ws_sb%d" % u) for u in range(2)]
         wi_sb = [keep.tile([P, 2, K], BF16, name="wi_sb%d" % u) for u in range(2)]
         wo_sb = keep.tile([P, V // P, K], BF16)
-        bout_bf = keep.tile([P, V], BF16)
+        b_rows = keep.tile([P, 2 * P], BF16)
+        bout_row = keep.tile([P, V], BF16)
+        ones = keep.tile([P, P], BF16)
+        nc.vector.memset(b_rows[:], 0.0)
+        nc.vector.memset(bout_row[:], 0.0)
+        nc.vector.memset(ones[:], 1.0)
+        nc.scalar.dma_start(out=b_rows[0:2, :], in_=b_second.rearrange("(u k) -> u k", u=2))
+        nc.scalar.dma_start(out=b_rows[2:4, :], in_=b_int.rearrange("(u k) -> u k", u=2))
+        nc.scalar.dma_start(out=bout_row[0:1, :], in_=b_out.rearrange("(o v) -> o v", o=1))
 
         def load_weight(w_sb, w, u):
             nc.sync.dma_start(
@@ -74,19 +82,10 @@ def tile_smcrossbaby_1_pb_t_kernel(
         load_y(2)
         nc.sync.dma_start(out=wo_sb[:], in_=w_out.rearrange("(c p) m -> p c m", p=P))
         load_f(1)
-        nc.sync.dma_start(out=bout_bf[:], in_=b_out.partition_broadcast(P))
         for g in range(2, N_GROUPS):
             load_f(g)
             if g + 1 < N_GROUPS:
                 load_y(g + 1)
-
-        bs_bf = keep.tile([P, PACK], BF16)
-        bi_bf = keep.tile([P, PACK], BF16)
-        for b_bf, b_dram in ((bs_bf, b_second), (bi_bf, b_int)):
-            nc.scalar.dma_start(
-                out=b_bf[:].rearrange("p (u e) -> p u e", e=2),
-                in_=b_dram.rearrange("(u p e) -> p u e", u=2, e=2),
-            )
 
         def regroup_pair(grouped, pair, rows_sb, chunk, copy_out):
             words = psum_words.tile([P, 2, 2 * P], F32, tag="words")
@@ -219,6 +218,11 @@ def tile_smcrossbaby_1_pb_t_kernel(
         regroup_y(0, [nc.vector.tensor_copy])
         regroup_pair(ws_grouped, 0, ws_sb[0], 0, nc.scalar.copy)
         quantise_y(0)
+        b_words = psum_words.tile([P, P], F32, tag="words")
+        nc.tensor.transpose(b_words[:], b_rows[:].bitcast(F32), ident[:])
+        b_cols = keep.tile([P, 2 * PACK], BF16)
+        nc.vector.tensor_copy(out=b_cols[:].bitcast(F32), in_=b_words[:, 0:PACK])
+        bs_bf, bi_bf = b_cols[:, 0:PACK], b_cols[:, PACK : 2 * PACK]
         regroup_pair(ws_grouped, 1, ws_sb[1], 0, nc.vector.tensor_copy)
         quantise(ws_q, ws_grouped, 0, 2 * P)
         regroup_pair(wi_grouped, 0, wi_sb[0], 0, nc.scalar.copy)
@@ -267,6 +271,10 @@ def tile_smcrossbaby_1_pb_t_kernel(
                 if r + 2 < N_GROUPS:
                     regroup_y(r + 2, [nc.vector.tensor_copy if r == 0 else nc.scalar.copy, nc.scalar.copy])
                 if r == 0:
+                    bout_bank = psum_words.tile([P, V], F32, tag="words")
+                    nc.tensor.matmul(bout_bank[:], lhsT=ones[:], rhs=bout_row[:], start=True, stop=True)
+                    bout_bf = keep.tile([P, V], BF16)
+                    nc.vector.tensor_copy(out=bout_bf[:], in_=bout_bank[:])
                     wo_grouped, wo_q = new_grouped(V), new_quantised(V, "wo")
                     regroup_pair(wo_grouped, 0, wo_sb, 0, nc.vector.tensor_copy)
                 if r > 0:

@@ -20,10 +20,8 @@ SIZES = (256, 512, 512, 512, 512, 512, 512, 512, 256)
 N_GROUPS = len(SIZES)
 STARTS = tuple(sum(SIZES[:g]) for g in range(N_GROUPS))
 BANK = 512
-GPSIMD_COLS = {512: 192, 256: 96}
+GPSIMD_COLS = 224
 RUN = 4
-GATE_LAG = 1
-HEAD_LAG = 2
 
 FLOPS = 2 * BATCH * K * (K + K + V)
 
@@ -36,7 +34,8 @@ def tile_smcrossbaby_1_pb_t_kernel(
         ctx.enter_context(tc.manual_schedule())
         keep = ctx.enter_context(tc.tile_pool(name="keep", bufs=1))
         work = ctx.enter_context(tc.tile_pool(name="work", bufs=2))
-        psum_words = ctx.enter_context(tc.psum_pool(name="psum_words", bufs=4))
+        psum_y = ctx.enter_context(tc.psum_pool(name="psum_y", bufs=2))
+        psum_first = ctx.enter_context(tc.psum_pool(name="psum_first", bufs=2))
         psum_acc = ctx.enter_context(tc.psum_pool(name="psum_acc", bufs=3))
         psum_head = ctx.enter_context(tc.psum_pool(name="psum_head", bufs=1))
 
@@ -57,9 +56,6 @@ def tile_smcrossbaby_1_pb_t_kernel(
         nc.vector.memset(b_rows[:], 0.0)
         nc.vector.memset(bout_row[:], 0.0)
         nc.vector.memset(ones[:], 1.0)
-        nc.scalar.dma_start(out=b_rows[0:2, :], in_=b_second.rearrange("(u k) -> u k", u=2))
-        nc.scalar.dma_start(out=b_rows[2:4, :], in_=b_int.rearrange("(u k) -> u k", u=2))
-        nc.scalar.dma_start(out=bout_row[0:1, :], in_=b_out.rearrange("(o v) -> o v", o=1))
 
         def load_weight(w_sb, w, u):
             nc.sync.dma_start(
@@ -74,6 +70,9 @@ def tile_smcrossbaby_1_pb_t_kernel(
 
         load_y(0)
         load_weight(ws_sb, w_second, 0)
+        nc.sync.dma_start(out=b_rows[0:2, :], in_=b_second.rearrange("(u k) -> u k", u=2))
+        nc.sync.dma_start(out=b_rows[2:4, :], in_=b_int.rearrange("(u k) -> u k", u=2))
+        nc.sync.dma_start(out=bout_row[0:1, :], in_=b_out.rearrange("(o v) -> o v", o=1))
         load_weight(ws_sb, w_second, 1)
         load_weight(wi_sb, w_int, 0)
         load_weight(wi_sb, w_int, 1)
@@ -87,8 +86,8 @@ def tile_smcrossbaby_1_pb_t_kernel(
             if g + 1 < N_GROUPS:
                 load_y(g + 1)
 
-        def regroup_pair(grouped, pair, rows_sb, chunk, copy_out):
-            words = psum_words.tile([P, 2, 2 * P], F32, tag="words")
+        def regroup_pair(bank_pool, grouped, pair, rows_sb, chunk, copy_out):
+            words = bank_pool.tile([P, 2, 2 * P], F32, tag="bank")
             for c in range(2):
                 for u in range(2):
                     nc.tensor.transpose(
@@ -137,7 +136,7 @@ def tile_smcrossbaby_1_pb_t_kernel(
         def first_words(g):
             banks = []
             for u in range(2):
-                f_words = psum_words.tile([P, SIZES[g]], F32, tag="words")
+                f_words = psum_first.tile([P, SIZES[g]], F32, tag="bank")
                 for c in range(SIZES[g] // P):
                     nc.tensor.transpose(
                         f_words[:, c * P : (c + 1) * P],
@@ -145,45 +144,39 @@ def tile_smcrossbaby_1_pb_t_kernel(
                         ident[:],
                     )
                 banks.append(f_words)
-            return banks
+            first_banks[g] = banks
 
-        def part_columns(g, h):
-            cut = SIZES[g] - GPSIMD_COLS[SIZES[g]]
-            return slice(0, cut) if h == 0 else slice(cut, SIZES[g])
-
-        def times_first(g, product, second, f_banks, h):
-            cols = part_columns(g, h)
+        def times_first(g, cols):
             for u in range(2):
                 nc.vector.tensor_tensor(
-                    out=product[:, 2 * u : 2 * u + 2, cols],
-                    in0=second[:, 2 * u : 2 * u + 2, cols],
-                    in1=f_banks[u][:].bitcast(BF16).rearrange("p (b e) -> p e b", e=2)[:, :, cols],
+                    out=product[g][:, 2 * u : 2 * u + 2, cols],
+                    in0=second[g][:, 2 * u : 2 * u + 2, cols],
+                    in1=first_banks[g][u][:].bitcast(BF16).rearrange("p (b e) -> p e b", e=2)[:, :, cols],
                     op=MULT,
                 )
 
-        def plus_inter(engine, g, z_grouped, product, inter, h):
-            cols = part_columns(g, h)
+        def plus_inter(engine, g, cols):
             engine.tensor_tensor(
-                out=z_grouped[:, cols, :].rearrange("p (c i) t -> p c t i", i=RUN),
-                in0=product[:, :, cols].rearrange("p t (c i) -> p c t i", i=RUN),
-                in1=inter[:, :, cols].rearrange("p t (c i) -> p c t i", i=RUN),
+                out=z_grouped[g][:, cols, :].rearrange("p (c i) t -> p c t i", i=RUN),
+                in0=product[g][:, :, cols].rearrange("p t (c i) -> p c t i", i=RUN),
+                in1=inter[g][:, :, cols].rearrange("p t (c i) -> p c t i", i=RUN),
                 op=ADD,
             )
 
-        def quantise_z(g, z_grouped, start, cols):
+        def quantise_z(g):
+            z_codes = work.tile([P, SIZES[g]], U32, align_bytes=64)
+            z_scales = work.tile([P, SIZES[g]], U8, align_bytes=64)
+            z_q[g] = (z_codes, z_scales)
             nc.vector.quantize_mx(
-                out=z_q[g][0][:, start : start + cols].bitcast(FP8X4),
-                scales=z_q[g][1][:, start : start + cols],
-                in_=z_grouped[:, start : start + cols, :].rearrange("p b t -> p (b t)"),
+                out=z_codes[:].bitcast(FP8X4), scales=z_scales[:], in_=z_grouped[g][:].rearrange("p b t -> p (b t)")
             )
 
-        def head_products(g, h):
-            chunks = SIZES[g] // P // 2
-            head = psum_head.tile([P, chunks, V], F32, tag="head")
-            for c in range(chunks):
-                j = chunks * h + c
+        def head(g, h):
+            bank = psum_head.tile([P, 2, V], F32, tag="bank")
+            for c in range(2):
+                j = 2 * h + c
                 nc.tensor.matmul_mx(
-                    out=head[:, c, :],
+                    out=bank[:, c, :],
                     lhsT=z_q[g][0][:, j * P : (j + 1) * P].bitcast(FP8X4),
                     lhsT_scale=z_q[g][1][:, j * P : (j + 1) * P],
                     rhs=wo_q[0][:].bitcast(FP8X4),
@@ -191,99 +184,108 @@ def tile_smcrossbaby_1_pb_t_kernel(
                     start=True,
                     stop=True,
                 )
-            return head
-
-        def add_b_out_and_store(g, head, h):
-            chunks = SIZES[g] // P // 2
-            out_sb = work.tile([P, chunks, V], F32, bufs=4, tag="out")
+            out_sb = work.tile([P, 2, V], F32, bufs=4, tag="out")
             nc.vector.tensor_tensor(
-                out=out_sb[:], in0=head[:], in1=bout_bf[:].unsqueeze(1).to_broadcast([P, chunks, V]), op=ADD
+                out=out_sb[:], in0=bank[:], in1=bout_bf[:].unsqueeze(1).to_broadcast([P, 2, V]), op=ADD
             )
-            nc.sync.dma_start(out=group_rows(out, g)[:, chunks * h : chunks * (h + 1), :], in_=out_sb[:])
+            nc.sync.dma_start(out=group_rows(out, g)[:, 2 * h : 2 * h + 2, :], in_=out_sb[:])
 
-        y_grouped, y_q = {}, {}
+        def start_group(g):
+            second[g] = work.tile([P, PACK, SIZES[g]], F32, tag="second", name="second")
+            inter[g] = work.tile([P, PACK, SIZES[g]], F32, tag="inter", name="inter")
+
+        def start_gate(g):
+            product[g] = work.tile([P, PACK, SIZES[g]], F32, tag="product", name="product")
+            z_grouped[g] = work.tile([P, SIZES[g], PACK], BF16, align_bytes=64, tag="z", name="z_grouped")
 
         def regroup_y(g, copies):
             y_grouped[g] = new_grouped(SIZES[g])
             for pair in range(SIZES[g] // (2 * P)):
-                regroup_pair(y_grouped[g], pair, y_sb[g], 2 * pair, copies[pair])
+                regroup_pair(psum_y, y_grouped[g], pair, y_sb[g], 2 * pair, copies[pair])
 
         def quantise_y(g):
             y_q[g] = new_quantised(SIZES[g], "y%d" % g)
             quantise(y_q[g], y_grouped[g], 0, SIZES[g])
 
+        y_grouped, y_q, second, inter, first_banks = {}, {}, {}, {}, {}
+        product, z_grouped, z_q = {}, {}, {}
+        by_scalar, by_vector = nc.scalar.copy, nc.vector.tensor_copy
+
         ws_grouped, ws_q = new_grouped(K), new_quantised(K, "ws")
         wi_grouped = keep.tile([P, K * PACK], BF16, align_bytes=64)
         wi_q = new_quantised(K, "wi")
-        regroup_y(0, [nc.vector.tensor_copy])
-        regroup_pair(ws_grouped, 0, ws_sb[0], 0, nc.scalar.copy)
+        regroup_y(0, [by_vector])
+        regroup_pair(psum_first, ws_grouped, 0, ws_sb[0], 0, by_scalar)
         quantise_y(0)
-        b_words = psum_words.tile([P, P], F32, tag="words")
+        regroup_pair(psum_first, ws_grouped, 1, ws_sb[1], 0, by_vector)
+        quantise(ws_q, ws_grouped, 0, 2 * P)
+        regroup_pair(psum_y, wi_grouped, 0, wi_sb[0], 0, by_scalar)
+        quantise(ws_q, ws_grouped, 2 * P, 2 * P)
+        b_words = psum_head.tile([P, P], F32, tag="bank")
         nc.tensor.transpose(b_words[:], b_rows[:].bitcast(F32), ident[:])
         b_cols = keep.tile([P, 2 * PACK], BF16)
         nc.vector.tensor_copy(out=b_cols[:].bitcast(F32), in_=b_words[:, 0:PACK])
         bs_bf, bi_bf = b_cols[:, 0:PACK], b_cols[:, PACK : 2 * PACK]
-        regroup_pair(ws_grouped, 1, ws_sb[1], 0, nc.vector.tensor_copy)
-        quantise(ws_q, ws_grouped, 0, 2 * P)
-        regroup_pair(wi_grouped, 0, wi_sb[0], 0, nc.scalar.copy)
-        quantise(ws_q, ws_grouped, 2 * P, 2 * P)
-        regroup_pair(wi_grouped, 1, wi_sb[1], 0, nc.vector.tensor_copy)
+        regroup_pair(psum_y, wi_grouped, 1, wi_sb[1], 0, by_vector)
         quantise(wi_q, wi_grouped, 0, 2 * P)
         quantise(wi_q, wi_grouped, 2 * P, 2 * P)
 
-        stage1 = {}
-        z_q = {}
-        LAST = N_GROUPS - 1
-        for r in range(N_GROUPS + HEAD_LAG):
-            gate, ahead = r - GATE_LAG, r - HEAD_LAG
-            in_stage1, in_gate, in_head = r < N_GROUPS, 0 <= gate < N_GROUPS, 0 <= ahead
-            if in_stage1:
-                new_second = work.tile([P, PACK, SIZES[r]], F32, tag="second")
-                new_inter = work.tile([P, PACK, SIZES[r]], F32, tag="inter")
-                relu_of_product(r, ws_q, bs_bf, new_second, (0, 1))
-            if in_gate:
-                second, inter, f_banks = stage1[gate]
-                product = work.tile([P, PACK, SIZES[gate]], F32, tag="product")
-                z_grouped = work.tile([P, SIZES[gate], PACK], BF16, align_bytes=64, tag="z")
-                times_first(gate, product, second, f_banks, 1)
-                plus_inter(nc.gpsimd, gate, z_grouped, product, inter, 1)
-            if in_head:
-                head = head_products(ahead, 0)
-                add_b_out_and_store(ahead, head, 0)
-            if in_stage1:
-                relu_of_product(r, ws_q, bs_bf, new_second, (2, 3))
-            if r == 0:
-                regroup_y(1, [nc.scalar.copy, nc.vector.tensor_copy])
-                quantise_y(1)
-            if in_gate:
-                times_first(gate, product, second, f_banks, 0)
-            if in_head:
-                head = head_products(ahead, 1)
-                add_b_out_and_store(ahead, head, 1)
-            if in_gate:
-                plus_inter(nc.vector, gate, z_grouped, product, inter, 0)
-            if 1 < r + 1 < N_GROUPS:
-                quantise_y(r + 1)
-            if in_stage1:
-                relu_of_product(r, wi_q, bi_bf, new_inter, range(PACK))
-                if r == 0:
-                    new_f_banks = first_words(r)
-                if r + 2 < N_GROUPS:
-                    regroup_y(r + 2, [nc.vector.tensor_copy if r == 0 else nc.scalar.copy, nc.scalar.copy])
-                if r == 0:
-                    bout_bank = psum_words.tile([P, V], F32, tag="words")
-                    nc.tensor.matmul(bout_bank[:], lhsT=ones[:], rhs=bout_row[:], start=True, stop=True)
-                    bout_bf = keep.tile([P, V], BF16)
-                    nc.vector.tensor_copy(out=bout_bf[:], in_=bout_bank[:])
-                    wo_grouped, wo_q = new_grouped(V), new_quantised(V, "wo")
-                    regroup_pair(wo_grouped, 0, wo_sb, 0, nc.vector.tensor_copy)
-                if r > 0:
-                    new_f_banks = first_words(r)
-                stage1[r] = (new_second, new_inter, new_f_banks)
-            if in_gate:
-                z_codes = work.tile([P, SIZES[gate]], U32, align_bytes=64)
-                z_scales = work.tile([P, SIZES[gate]], U8, align_bytes=64)
-                z_q[gate] = (z_codes, z_scales)
-                quantise_z(gate, z_grouped, 0, SIZES[gate])
-            if r == 1:
-                quantise(wo_q, wo_grouped, 0, V)
+        start_group(0)
+        start_gate(0)
+        relu_of_product(0, ws_q, bs_bf, second[0], range(PACK))
+        regroup_y(1, [by_scalar, by_vector])
+        quantise_y(1)
+        first_words(0)
+        times_first(0, slice(0, SIZES[0]))
+        relu_of_product(0, wi_q, bi_bf, inter[0], range(PACK))
+
+        start_group(1)
+        relu_of_product(1, ws_q, bs_bf, second[1], (0, 1))
+        y_grouped[2] = new_grouped(SIZES[2])
+        regroup_pair(psum_y, y_grouped[2], 0, y_sb[2], 0, by_vector)
+        relu_of_product(1, ws_q, bs_bf, second[1], (2, 3))
+        plus_inter(nc.vector, 0, slice(0, SIZES[0]))
+        quantise_z(0)
+        regroup_pair(psum_y, y_grouped[2], 1, y_sb[2], 2, by_scalar)
+        first_words(1)
+        quantise_y(2)
+        wo_grouped, wo_q = new_grouped(V), new_quantised(V, "wo")
+        regroup_pair(psum_head, wo_grouped, 0, wo_sb, 0, by_scalar)
+        relu_of_product(1, wi_q, bi_bf, inter[1], range(PACK))
+        quantise(wo_q, wo_grouped, 0, V)
+        bout_bank = psum_head.tile([P, V], F32, tag="bank")
+        nc.tensor.matmul(bout_bank[:], lhsT=ones[:], rhs=bout_row[:], start=True, stop=True)
+        bout_bf = keep.tile([P, V], BF16)
+        nc.vector.tensor_copy(out=bout_bf[:], in_=bout_bank[:])
+        regroup_y(3, [by_scalar, by_scalar])
+
+        gpsimd_cols = slice(BANK - GPSIMD_COLS, BANK)
+        vector_cols = slice(0, BANK - GPSIMD_COLS)
+        for r in range(2, N_GROUPS):
+            start_group(r)
+            start_gate(r - 1)
+            relu_of_product(r, ws_q, bs_bf, second[r], (0, 1))
+            times_first(r - 1, gpsimd_cols)
+            plus_inter(nc.gpsimd, r - 1, gpsimd_cols)
+            head(r - 2, 0)
+            relu_of_product(r, ws_q, bs_bf, second[r], (2, 3))
+            if r + 2 < N_GROUPS:
+                regroup_y(r + 2, [by_scalar, by_scalar])
+            times_first(r - 1, vector_cols)
+            if SIZES[r - 2] == BANK:
+                head(r - 2, 1)
+            plus_inter(nc.vector, r - 1, vector_cols)
+            for g in range(len(y_q), min(r + 3, N_GROUPS)):
+                quantise_y(g)
+            quantise_z(r - 1)
+            relu_of_product(r, wi_q, bi_bf, inter[r], range(PACK))
+            first_words(r)
+
+        last = N_GROUPS - 1
+        start_gate(last)
+        times_first(last, slice(0, SIZES[last]))
+        head(last - 1, 0)
+        plus_inter(nc.vector, last, slice(0, SIZES[last]))
+        head(last - 1, 1)
+        quantise_z(last)
+        head(last, 0)

@@ -20,7 +20,7 @@ SIZES = (256, 512, 512, 512, 512, 512, 512, 512, 256)
 N_GROUPS = len(SIZES)
 STARTS = tuple(sum(SIZES[:g]) for g in range(N_GROUPS))
 BANK = 512
-GPSIMD_COLS = 224
+PARTS = {"lower": (0, 256, 2), "upper": (256, 256, 1)}
 RUN = 4
 
 FLOPS = 2 * BATCH * K * (K + K + V)
@@ -133,46 +133,51 @@ def tile_smcrossbaby_1_pb_t_kernel(
                     out=result[:, t, :], in_=acc[:], func=RELU, bias=w_bias[:, t : t + 1], scale=1.0
                 )
 
-        def first_words(g):
-            banks = []
-            for u in range(2):
-                f_words = psum_first.tile([P, SIZES[g]], F32, tag="bank")
-                for c in range(SIZES[g] // P):
-                    nc.tensor.transpose(
-                        f_words[:, c * P : (c + 1) * P],
-                        f_sb[g][:, c, :].bitcast(F32)[:, u * P : (u + 1) * P],
-                        ident[:],
-                    )
-                banks.append(f_words)
-            first_banks[g] = banks
-
-        def times_first(g, cols):
-            for u in range(2):
-                nc.vector.tensor_tensor(
-                    out=product[g][:, 2 * u : 2 * u + 2, cols],
-                    in0=second[g][:, 2 * u : 2 * u + 2, cols],
-                    in1=first_banks[g][u][:].bitcast(BF16).rearrange("p (b e) -> p e b", e=2)[:, :, cols],
-                    op=MULT,
+        def first_words(g, u):
+            f_words = psum_first.tile([P, SIZES[g]], F32, tag="bank")
+            for c in range(SIZES[g] // P):
+                nc.tensor.transpose(
+                    f_words[:, c * P : (c + 1) * P],
+                    f_sb[g][:, c, :].bitcast(F32)[:, u * P : (u + 1) * P],
+                    ident[:],
                 )
+            first_banks[g, u] = f_words
 
-        def plus_inter(engine, g, cols):
+        def times_first(g, u):
+            if u == 0:
+                product[g] = work.tile([P, PACK, SIZES[g]], F32, tag="product", name="product")
+            nc.vector.tensor_tensor(
+                out=product[g][:, 2 * u : 2 * u + 2, :],
+                in0=second[g][:, 2 * u : 2 * u + 2, :],
+                in1=first_banks[g, u][:].bitcast(BF16).rearrange("p (b e) -> p e b", e=2),
+                op=MULT,
+            )
+
+        def plus_inter(engine, g, part):
+            start, cols, bufs = PARTS[part]
+            z_grouped = work.tile([P, cols, PACK], BF16, align_bytes=64, tag="z_" + part, bufs=bufs)
             engine.tensor_tensor(
-                out=z_grouped[g][:, cols, :].rearrange("p (c i) t -> p c t i", i=RUN),
-                in0=product[g][:, :, cols].rearrange("p t (c i) -> p c t i", i=RUN),
-                in1=inter[g][:, :, cols].rearrange("p t (c i) -> p c t i", i=RUN),
+                out=z_grouped[:].rearrange("p (c i) t -> p c t i", i=RUN),
+                in0=product[g][:, :, start : start + cols].rearrange("p t (c i) -> p c t i", i=RUN),
+                in1=inter[g][:, :, start : start + cols].rearrange("p t (c i) -> p c t i", i=RUN),
                 op=ADD,
             )
+            z_rows[g, part] = z_grouped
 
-        def quantise_z(g):
-            z_codes = work.tile([P, SIZES[g]], U32, align_bytes=64)
-            z_scales = work.tile([P, SIZES[g]], U8, align_bytes=64)
-            z_q[g] = (z_codes, z_scales)
+        def quantise_z(g, part):
+            start, cols, bufs = PARTS[part]
+            if g not in z_q:
+                z_codes = work.tile([P, SIZES[g]], U32, align_bytes=64, bufs=3)
+                z_scales = work.tile([P, SIZES[g]], U8, align_bytes=64, bufs=3)
+                z_q[g] = (z_codes, z_scales)
             nc.vector.quantize_mx(
-                out=z_codes[:].bitcast(FP8X4), scales=z_scales[:], in_=z_grouped[g][:].rearrange("p b t -> p (b t)")
+                out=z_q[g][0][:, start : start + cols].bitcast(FP8X4),
+                scales=z_q[g][1][:, start : start + cols],
+                in_=z_rows[g, part][:].rearrange("p b t -> p (b t)"),
             )
 
-        def head(g, h):
-            bank = psum_head.tile([P, 2, V], F32, tag="bank")
+        def head(g, h, pool):
+            bank = pool.tile([P, 2, V], F32, tag="bank")
             for c in range(2):
                 j = 2 * h + c
                 nc.tensor.matmul_mx(
@@ -192,29 +197,32 @@ def tile_smcrossbaby_1_pb_t_kernel(
 
         def start_group(g):
             second[g] = work.tile([P, PACK, SIZES[g]], F32, tag="second", name="second")
-            inter[g] = work.tile([P, PACK, SIZES[g]], F32, tag="inter", name="inter")
+            inter[g] = work.tile([P, PACK, SIZES[g]], F32, tag="inter", name="inter", bufs=3)
 
-        def start_gate(g):
-            product[g] = work.tile([P, PACK, SIZES[g]], F32, tag="product", name="product")
-            z_grouped[g] = work.tile([P, SIZES[g], PACK], BF16, align_bytes=64, tag="z", name="z_grouped")
-
-        def regroup_y(g, copies):
-            y_grouped[g] = new_grouped(SIZES[g])
-            for pair in range(SIZES[g] // (2 * P)):
-                regroup_pair(psum_y, y_grouped[g], pair, y_sb[g], 2 * pair, copies[pair])
+        def regroup_y(g, pair, copy_out):
+            if pair == 0:
+                y_grouped[g] = new_grouped(SIZES[g])
+            regroup_pair(psum_y, y_grouped[g], pair, y_sb[g], 2 * pair, copy_out)
 
         def quantise_y(g):
             y_q[g] = new_quantised(SIZES[g], "y%d" % g)
             quantise(y_q[g], y_grouped[g], 0, SIZES[g])
 
         y_grouped, y_q, second, inter, first_banks = {}, {}, {}, {}, {}
-        product, z_grouped, z_q = {}, {}, {}
+        product, z_rows, z_q = {}, {}, {}
         by_scalar, by_vector = nc.scalar.copy, nc.vector.tensor_copy
+
+        def second_of(g, ts):
+            relu_of_product(g, ws_q, bs_bf, second[g], ts)
+
+        def inter_of(g, ts):
+            relu_of_product(g, wi_q, bi_bf, inter[g], ts)
 
         ws_grouped, ws_q = new_grouped(K), new_quantised(K, "ws")
         wi_grouped = keep.tile([P, K * PACK], BF16, align_bytes=64)
         wi_q = new_quantised(K, "wi")
-        regroup_y(0, [by_vector])
+        start_group(0)
+        regroup_y(0, 0, by_vector)
         regroup_pair(psum_first, ws_grouped, 0, ws_sb[0], 0, by_scalar)
         quantise_y(0)
         regroup_pair(psum_first, ws_grouped, 1, ws_sb[1], 0, by_vector)
@@ -229,63 +237,75 @@ def tile_smcrossbaby_1_pb_t_kernel(
         regroup_pair(psum_y, wi_grouped, 1, wi_sb[1], 0, by_vector)
         quantise(wi_q, wi_grouped, 0, 2 * P)
         quantise(wi_q, wi_grouped, 2 * P, 2 * P)
-
-        start_group(0)
-        start_gate(0)
-        relu_of_product(0, ws_q, bs_bf, second[0], range(PACK))
-        regroup_y(1, [by_scalar, by_vector])
+        second_of(0, range(PACK))
+        regroup_y(1, 0, by_scalar)
+        regroup_y(1, 1, by_vector)
         quantise_y(1)
-        first_words(0)
-        times_first(0, slice(0, SIZES[0]))
-        relu_of_product(0, wi_q, bi_bf, inter[0], range(PACK))
-
-        start_group(1)
-        relu_of_product(1, ws_q, bs_bf, second[1], (0, 1))
-        y_grouped[2] = new_grouped(SIZES[2])
-        regroup_pair(psum_y, y_grouped[2], 0, y_sb[2], 0, by_vector)
-        relu_of_product(1, ws_q, bs_bf, second[1], (2, 3))
-        plus_inter(nc.vector, 0, slice(0, SIZES[0]))
-        quantise_z(0)
-        regroup_pair(psum_y, y_grouped[2], 1, y_sb[2], 2, by_scalar)
-        first_words(1)
-        quantise_y(2)
-        wo_grouped, wo_q = new_grouped(V), new_quantised(V, "wo")
-        regroup_pair(psum_head, wo_grouped, 0, wo_sb, 0, by_scalar)
-        relu_of_product(1, wi_q, bi_bf, inter[1], range(PACK))
-        quantise(wo_q, wo_grouped, 0, V)
+        first_words(0, 0)
+        first_words(0, 1)
+        times_first(0, 0)
+        times_first(0, 1)
+        inter_of(0, range(PACK))
         bout_bank = psum_head.tile([P, V], F32, tag="bank")
         nc.tensor.matmul(bout_bank[:], lhsT=ones[:], rhs=bout_row[:], start=True, stop=True)
         bout_bf = keep.tile([P, V], BF16)
         nc.vector.tensor_copy(out=bout_bf[:], in_=bout_bank[:])
-        regroup_y(3, [by_scalar, by_scalar])
 
-        gpsimd_cols = slice(BANK - GPSIMD_COLS, BANK)
-        vector_cols = slice(0, BANK - GPSIMD_COLS)
+        start_group(1)
+        second_of(1, (0, 1))
+        regroup_y(2, 0, by_vector)
+        second_of(1, (2, 3))
+        plus_inter(nc.vector, 0, "lower")
+        quantise_z(0, "lower")
+        first_words(1, 0)
+        wo_grouped, wo_q = new_grouped(V), new_quantised(V, "wo")
+        regroup_pair(psum_head, wo_grouped, 0, wo_sb, 0, by_vector)
+        regroup_y(2, 1, by_scalar)
+        inter_of(1, (0, 1))
+        first_words(1, 1)
+        quantise_y(2)
+        inter_of(1, (2, 3))
+        quantise(wo_q, wo_grouped, 0, V)
+        times_first(1, 0)
+        head(0, 0, psum_head)
+        regroup_y(3, 0, by_scalar)
+        regroup_y(3, 1, by_scalar)
+
         for r in range(2, N_GROUPS):
             start_group(r)
-            start_gate(r - 1)
-            relu_of_product(r, ws_q, bs_bf, second[r], (0, 1))
-            times_first(r - 1, gpsimd_cols)
-            plus_inter(nc.gpsimd, r - 1, gpsimd_cols)
-            head(r - 2, 0)
-            relu_of_product(r, ws_q, bs_bf, second[r], (2, 3))
+            second_of(r, (0, 1))
+            if r > 2:
+                plus_inter(nc.gpsimd, r - 2, "upper")
+            if r > 2:
+                times_first(r - 1, 0)
+                head(r - 2, 0, psum_head)
             if r + 2 < N_GROUPS:
-                regroup_y(r + 2, [by_scalar, by_scalar])
-            times_first(r - 1, vector_cols)
-            if SIZES[r - 2] == BANK:
-                head(r - 2, 1)
-            plus_inter(nc.vector, r - 1, vector_cols)
+                regroup_y(r + 2, 0, by_scalar)
+            second_of(r, (2, 3))
+            times_first(r - 1, 1)
+            if r > 3:
+                head(r - 3, 1, psum_head)
+            if r + 2 < N_GROUPS and SIZES[r + 2] == BANK:
+                regroup_y(r + 2, 1, by_vector if r == 2 else by_scalar)
+            inter_of(r, (0, 1))
+            first_words(r, 0)
+            plus_inter(nc.vector, r - 1, "lower")
             for g in range(len(y_q), min(r + 3, N_GROUPS)):
                 quantise_y(g)
-            quantise_z(r - 1)
-            relu_of_product(r, wi_q, bi_bf, inter[r], range(PACK))
-            first_words(r)
+            if r > 2:
+                quantise_z(r - 2, "upper")
+            quantise_z(r - 1, "lower")
+            inter_of(r, (2, 3))
+            first_words(r, 1)
 
         last = N_GROUPS - 1
-        start_gate(last)
-        times_first(last, slice(0, SIZES[last]))
-        head(last - 1, 0)
-        plus_inter(nc.vector, last, slice(0, SIZES[last]))
-        head(last - 1, 1)
-        quantise_z(last)
-        head(last, 0)
+        plus_inter(nc.gpsimd, last - 1, "upper")
+        times_first(last, 0)
+        times_first(last, 1)
+        head(last - 1, 0, psum_head)
+        head(last - 2, 1, psum_y)
+        plus_inter(nc.vector, last, "lower")
+        quantise_z(last, "lower")
+        quantise_z(last - 1, "upper")
+        head(last, 0, psum_y)
+        head(last - 1, 1, psum_head)

@@ -53,6 +53,11 @@ def tile_smcrossbaby_1_pb_t_kernel(
         b_rows = keep.tile([P, 2 * P], BF16)
         bout_row = keep.tile([P, V], BF16)
         ones = keep.tile([P, P], BF16)
+        ones_wide = keep.tile([P, BANK], BF16)
+        nc.vector.memset(ones_wide[:], 1.0)
+        warm = psum_acc.tile([P, BANK], F32, tag="acc")
+        for i in range(6):
+            nc.tensor.matmul(warm[:], lhsT=ones_wide[:, 0:P], rhs=ones_wide[:], start=True, stop=True)
         nc.vector.memset(b_rows[:], 0.0)
         nc.vector.memset(bout_row[:], 0.0)
         nc.vector.memset(ones[:], 1.0)
@@ -199,6 +204,23 @@ def tile_smcrossbaby_1_pb_t_kernel(
             second[g] = work.tile([P, PACK, SIZES[g]], F32, tag="second", name="second")
             inter[g] = work.tile([P, PACK, SIZES[g]], F32, tag="inter", name="inter", bufs=3)
 
+        def copy_pair(grouped, pair, words, copy_out):
+            copy_out(
+                out=grouped[:].bitcast(F32).rearrange("p (c u) -> p c u", u=2)[:, pair * 2 * P : (pair + 1) * 2 * P, :],
+                in_=words[:].rearrange("p u c -> p c u"),
+            )
+
+        def y_words(g, pair):
+            words = psum_y.tile([P, 2, 2 * P], F32, tag="bank")
+            for c in range(2):
+                for u in range(2):
+                    nc.tensor.transpose(
+                        words[:, u, c * P : (c + 1) * P],
+                        y_sb[g][:, 2 * pair + c, :].bitcast(F32)[:, u * P : (u + 1) * P],
+                        ident[:],
+                    )
+            return words
+
         def regroup_y(g, pair, copy_out):
             if pair == 0:
                 y_grouped[g] = new_grouped(SIZES[g])
@@ -238,6 +260,10 @@ def tile_smcrossbaby_1_pb_t_kernel(
         quantise(wi_q, wi_grouped, 0, 2 * P)
         quantise(wi_q, wi_grouped, 2 * P, 2 * P)
         second_of(0, range(PACK))
+        bout_bank = psum_head.tile([P, V], F32, tag="bank")
+        nc.tensor.matmul(bout_bank[:], lhsT=ones[:], rhs=bout_row[:], start=True, stop=True)
+        bout_bf = keep.tile([P, V], BF16)
+        nc.vector.tensor_copy(out=bout_bf[:], in_=bout_bank[:])
         regroup_y(1, 0, by_scalar)
         regroup_y(1, 1, by_vector)
         quantise_y(1)
@@ -246,10 +272,6 @@ def tile_smcrossbaby_1_pb_t_kernel(
         times_first(0, 0)
         times_first(0, 1)
         inter_of(0, range(PACK))
-        bout_bank = psum_head.tile([P, V], F32, tag="bank")
-        nc.tensor.matmul(bout_bank[:], lhsT=ones[:], rhs=bout_row[:], start=True, stop=True)
-        bout_bf = keep.tile([P, V], BF16)
-        nc.vector.tensor_copy(out=bout_bf[:], in_=bout_bank[:])
 
         start_group(1)
         second_of(1, (0, 1))
@@ -271,41 +293,64 @@ def tile_smcrossbaby_1_pb_t_kernel(
         regroup_y(3, 0, by_scalar)
         regroup_y(3, 1, by_scalar)
 
-        for r in range(2, N_GROUPS):
+        def large(g):
+            return 0 <= g < N_GROUPS and SIZES[g] == BANK
+
+        start_group(2)
+        second_of(2, (0, 1))
+        regroup_y(4, 0, by_scalar)
+        second_of(2, (2, 3))
+        late = y_words(4, 1)
+        times_first(1, 1)
+        plus_inter(nc.vector, 1, "lower")
+        quantise_y(3)
+        inter_of(2, (0, 1))
+        first_words(2, 0)
+        copy_pair(y_grouped[4], 1, late, by_vector)
+        quantise_z(1, "lower")
+        quantise_y(4)
+        inter_of(2, (2, 3))
+        first_words(2, 1)
+
+        for r in range(3, N_GROUPS):
             start_group(r)
             second_of(r, (0, 1))
             if r > 2:
-                plus_inter(nc.gpsimd, r - 2, "upper")
-            if r > 2:
+                if large(r - 2):
+                    plus_inter(nc.gpsimd, r - 2, "upper")
                 times_first(r - 1, 0)
                 head(r - 2, 0, psum_head)
             if r + 2 < N_GROUPS:
                 regroup_y(r + 2, 0, by_scalar)
             second_of(r, (2, 3))
             times_first(r - 1, 1)
-            if r > 3:
+            if large(r - 3):
                 head(r - 3, 1, psum_head)
-            if r + 2 < N_GROUPS and SIZES[r + 2] == BANK:
-                regroup_y(r + 2, 1, by_vector if r == 2 else by_scalar)
+            if large(r + 2):
+                regroup_y(r + 2, 1, by_scalar)
             inter_of(r, (0, 1))
             first_words(r, 0)
             plus_inter(nc.vector, r - 1, "lower")
-            for g in range(len(y_q), min(r + 3, N_GROUPS)):
-                quantise_y(g)
-            if r > 2:
+            if r + 2 < N_GROUPS:
+                quantise_y(r + 2)
+            if large(r - 2):
                 quantise_z(r - 2, "upper")
             quantise_z(r - 1, "lower")
             inter_of(r, (2, 3))
             first_words(r, 1)
 
         last = N_GROUPS - 1
-        plus_inter(nc.gpsimd, last - 1, "upper")
+        if large(last - 1):
+            plus_inter(nc.gpsimd, last - 1, "upper")
         times_first(last, 0)
         times_first(last, 1)
         head(last - 1, 0, psum_head)
-        head(last - 2, 1, psum_y)
+        if large(last - 2):
+            head(last - 2, 1, psum_y)
         plus_inter(nc.vector, last, "lower")
         quantise_z(last, "lower")
-        quantise_z(last - 1, "upper")
+        if large(last - 1):
+            quantise_z(last - 1, "upper")
         head(last, 0, psum_y)
-        head(last - 1, 1, psum_head)
+        if large(last - 1):
+            head(last - 1, 1, psum_head)

@@ -20,7 +20,9 @@ SIZES = (256, 512, 512, 512, 512, 512, 512, 512, 256)
 N_GROUPS = len(SIZES)
 STARTS = tuple(sum(SIZES[:g]) for g in range(N_GROUPS))
 BANK = 512
-PARTS = {"lower": (0, 256, 2), "upper": (256, 256, 1)}
+LOWER = 256
+UPPER = BANK - LOWER
+WARM = 14
 RUN = 4
 
 FLOPS = 2 * BATCH * K * (K + K + V)
@@ -53,14 +55,12 @@ def tile_smcrossbaby_1_pb_t_kernel(
         b_rows = keep.tile([P, 2 * P], BF16)
         bout_row = keep.tile([P, V], BF16)
         ones = keep.tile([P, P], BF16)
-        ones_wide = keep.tile([P, BANK], BF16)
-        nc.vector.memset(ones_wide[:], 1.0)
-        warm = psum_acc.tile([P, BANK], F32, tag="acc")
-        for i in range(6):
-            nc.tensor.matmul(warm[:], lhsT=ones_wide[:, 0:P], rhs=ones_wide[:], start=True, stop=True)
+        nc.vector.memset(ones[:], 1.0)
+        warm = psum_acc.tile([P, P], F32, tag="acc")
+        for i in range(WARM):
+            nc.tensor.matmul(warm[:], lhsT=ones[:], rhs=ones[:], start=True, stop=True)
         nc.vector.memset(b_rows[:], 0.0)
         nc.vector.memset(bout_row[:], 0.0)
-        nc.vector.memset(ones[:], 1.0)
 
         def load_weight(w_sb, w, u):
             nc.sync.dma_start(
@@ -158,37 +158,39 @@ def tile_smcrossbaby_1_pb_t_kernel(
                 op=MULT,
             )
 
-        def plus_inter(engine, g, part):
-            start, cols, bufs = PARTS[part]
-            z_grouped = work.tile([P, cols, PACK], BF16, align_bytes=64, tag="z_" + part, bufs=bufs)
+        def plus_inter(engine, g, cols, z_part):
             engine.tensor_tensor(
-                out=z_grouped[:].rearrange("p (c i) t -> p c t i", i=RUN),
-                in0=product[g][:, :, start : start + cols].rearrange("p t (c i) -> p c t i", i=RUN),
-                in1=inter[g][:, :, start : start + cols].rearrange("p t (c i) -> p c t i", i=RUN),
+                out=z_part.rearrange("p (c i) t -> p c t i", i=RUN),
+                in0=product[g][:, :, cols].rearrange("p t (c i) -> p c t i", i=RUN),
+                in1=inter[g][:, :, cols].rearrange("p t (c i) -> p c t i", i=RUN),
                 op=ADD,
             )
-            z_rows[g, part] = z_grouped
 
-        def quantise_z(g, part):
-            start, cols, bufs = PARTS[part]
-            if g not in z_q:
-                z_codes = work.tile([P, SIZES[g]], U32, align_bytes=64, bufs=3)
-                z_scales = work.tile([P, SIZES[g]], U8, align_bytes=64, bufs=3)
-                z_q[g] = (z_codes, z_scales)
+        def new_z():
+            z_grouped = work.tile([P, BANK, PACK], BF16, align_bytes=64, tag="z", bufs=1)
+            z_codes = work.tile([P, BANK], U32, align_bytes=64, bufs=3)
+            z_scales = work.tile([P, BANK], U8, align_bytes=64, bufs=3)
+            return z_grouped, z_codes, z_scales
+
+        def quantise_z(z, start, cols):
             nc.vector.quantize_mx(
-                out=z_q[g][0][:, start : start + cols].bitcast(FP8X4),
-                scales=z_q[g][1][:, start : start + cols],
-                in_=z_rows[g, part][:].rearrange("p b t -> p (b t)"),
+                out=z[1][:, start : start + cols].bitcast(FP8X4),
+                scales=z[2][:, start : start + cols],
+                in_=z[0][:, start : start + cols, :].rearrange("p b t -> p (b t)"),
             )
+
+        def place(g, first_chunk, z, start, cols):
+            for c in range(cols // P):
+                z_place[g, first_chunk + c] = (z[1], z[2], slice(start + c * P, start + (c + 1) * P))
 
         def head(g, h, pool):
             bank = pool.tile([P, 2, V], F32, tag="bank")
             for c in range(2):
-                j = 2 * h + c
+                codes, scales, cols = z_place[g, 2 * h + c]
                 nc.tensor.matmul_mx(
                     out=bank[:, c, :],
-                    lhsT=z_q[g][0][:, j * P : (j + 1) * P].bitcast(FP8X4),
-                    lhsT_scale=z_q[g][1][:, j * P : (j + 1) * P],
+                    lhsT=codes[:, cols].bitcast(FP8X4),
+                    lhsT_scale=scales[:, cols],
                     rhs=wo_q[0][:].bitcast(FP8X4),
                     rhs_scale=wo_q[1][:],
                     start=True,
@@ -231,7 +233,7 @@ def tile_smcrossbaby_1_pb_t_kernel(
             quantise(y_q[g], y_grouped[g], 0, SIZES[g])
 
         y_grouped, y_q, second, inter, first_banks = {}, {}, {}, {}, {}
-        product, z_rows, z_q = {}, {}, {}
+        product, z_place = {}, {}
         by_scalar, by_vector = nc.scalar.copy, nc.vector.tensor_copy
 
         def second_of(g, ts):
@@ -277,8 +279,10 @@ def tile_smcrossbaby_1_pb_t_kernel(
         second_of(1, (0, 1))
         regroup_y(2, 0, by_vector)
         second_of(1, (2, 3))
-        plus_inter(nc.vector, 0, "lower")
-        quantise_z(0, "lower")
+        z = new_z()
+        plus_inter(nc.vector, 0, slice(0, SIZES[0]), z[0][:, 0 : SIZES[0], :])
+        quantise_z(z, 0, SIZES[0])
+        place(0, 0, z, 0, SIZES[0])
         first_words(1, 0)
         wo_grouped, wo_q = new_grouped(V), new_quantised(V, "wo")
         regroup_pair(psum_head, wo_grouped, 0, wo_sb, 0, by_vector)
@@ -293,21 +297,20 @@ def tile_smcrossbaby_1_pb_t_kernel(
         regroup_y(3, 0, by_scalar)
         regroup_y(3, 1, by_scalar)
 
-        def large(g):
-            return 0 <= g < N_GROUPS and SIZES[g] == BANK
-
         start_group(2)
         second_of(2, (0, 1))
         regroup_y(4, 0, by_scalar)
         second_of(2, (2, 3))
-        late = y_words(4, 1)
+        late_words = y_words(4, 1)
         times_first(1, 1)
-        plus_inter(nc.vector, 1, "lower")
+        z = new_z()
+        plus_inter(nc.vector, 1, slice(0, LOWER), z[0][:, UPPER:BANK, :])
         quantise_y(3)
         inter_of(2, (0, 1))
         first_words(2, 0)
-        copy_pair(y_grouped[4], 1, late, by_vector)
-        quantise_z(1, "lower")
+        copy_pair(y_grouped[4], 1, late_words, by_vector)
+        quantise_z(z, UPPER, LOWER)
+        place(1, 0, z, UPPER, LOWER)
         quantise_y(4)
         inter_of(2, (2, 3))
         first_words(2, 1)
@@ -315,42 +318,45 @@ def tile_smcrossbaby_1_pb_t_kernel(
         for r in range(3, N_GROUPS):
             start_group(r)
             second_of(r, (0, 1))
-            if r > 2:
-                if large(r - 2):
-                    plus_inter(nc.gpsimd, r - 2, "upper")
-                times_first(r - 1, 0)
+            z = new_z()
+            plus_inter(nc.gpsimd, r - 2, slice(LOWER, BANK), z[0][:, 0:UPPER, :])
+            times_first(r - 1, 0)
+            if r + 2 < N_GROUPS and r > 3:
                 head(r - 2, 0, psum_head)
             if r + 2 < N_GROUPS:
                 regroup_y(r + 2, 0, by_scalar)
             second_of(r, (2, 3))
             times_first(r - 1, 1)
-            if large(r - 3):
+            if r == 3:
+                head(1, 0, psum_head)
+            if r > 3:
                 head(r - 3, 1, psum_head)
-            if large(r + 2):
+            if r + 2 < N_GROUPS and SIZES[r + 2] == BANK:
                 regroup_y(r + 2, 1, by_scalar)
             inter_of(r, (0, 1))
             first_words(r, 0)
-            plus_inter(nc.vector, r - 1, "lower")
+            plus_inter(nc.vector, r - 1, slice(0, LOWER), z[0][:, UPPER:BANK, :])
             if r + 2 < N_GROUPS:
                 quantise_y(r + 2)
-            if large(r - 2):
-                quantise_z(r - 2, "upper")
-            quantise_z(r - 1, "lower")
+            else:
+                head(r - 2, 0, psum_head)
+            quantise_z(z, 0, BANK)
+            place(r - 2, LOWER // P, z, 0, UPPER)
+            place(r - 1, 0, z, UPPER, LOWER)
             inter_of(r, (2, 3))
             first_words(r, 1)
 
         last = N_GROUPS - 1
-        if large(last - 1):
-            plus_inter(nc.gpsimd, last - 1, "upper")
+        z = new_z()
+        plus_inter(nc.gpsimd, last - 1, slice(LOWER, BANK), z[0][:, 0:UPPER, :])
+        place(last - 1, LOWER // P, z, 0, UPPER)
         times_first(last, 0)
         times_first(last, 1)
         head(last - 1, 0, psum_head)
-        if large(last - 2):
-            head(last - 2, 1, psum_y)
-        plus_inter(nc.vector, last, "lower")
-        quantise_z(last, "lower")
-        if large(last - 1):
-            quantise_z(last - 1, "upper")
+        head(last - 2, 1, psum_y)
+        plus_inter(nc.vector, last, slice(0, SIZES[last]), z[0][:, UPPER:BANK, :])
+        quantise_z(z, 0, UPPER)
+        quantise_z(z, UPPER, SIZES[last])
+        place(last, 0, z, UPPER, SIZES[last])
         head(last, 0, psum_y)
-        if large(last - 1):
-            head(last - 1, 1, psum_head)
+        head(last - 1, 1, psum_head)

@@ -23,7 +23,7 @@ BANK = 512
 LOWER = 256
 UPPER = BANK - LOWER
 WARM = 14
-RUN = 4
+RUN = 8
 
 FLOPS = 2 * BATCH * K * (K + K + V)
 

@@ -202,6 +202,23 @@ def tile_smcrossbaby_1_pb_t_kernel(
             )
             nc.sync.dma_start(out=group_rows(out, g)[:, 2 * h : 2 * h + 2, :], in_=out_sb[:])
 
+        def last_head(g):
+            for c, pool in ((0, psum_y), (1, psum_first)):
+                bank = pool.tile([P, V], F32, tag="bank")
+                codes, scales, cols = z_place[g, c]
+                nc.tensor.matmul_mx(
+                    out=bank[:],
+                    lhsT=codes[:, cols].bitcast(FP8X4),
+                    lhsT_scale=scales[:, cols],
+                    rhs=wo_q[0][:].bitcast(FP8X4),
+                    rhs_scale=wo_q[1][:],
+                    start=True,
+                    stop=True,
+                )
+                out_sb = work.tile([P, V], F32, tag="last_out")
+                nc.vector.tensor_tensor(out=out_sb[:], in0=bank[:], in1=bout_bf[:], op=ADD)
+                nc.sync.dma_start(out=group_rows(out, g)[:, c, :], in_=out_sb[:])
+
         def start_group(g):
             second[g] = work.tile([P, PACK, SIZES[g]], F32, tag="second", name="second")
             inter[g] = work.tile([P, PACK, SIZES[g]], F32, tag="inter", name="inter", bufs=3)
@@ -358,5 +375,5 @@ def tile_smcrossbaby_1_pb_t_kernel(
         quantise_z(z, 0, UPPER)
         quantise_z(z, UPPER, SIZES[last])
         place(last, 0, z, UPPER, SIZES[last])
-        head(last, 0, psum_y)
         head(last - 1, 1, psum_head)
+        last_head(last)

@@ -20,8 +20,8 @@ SIZES = (256, 512, 512, 512, 512, 512, 512, 512, 256)
 N_GROUPS = len(SIZES)
 STARTS = tuple(sum(SIZES[:g]) for g in range(N_GROUPS))
 BANK = 512
-LOWER = 256
-UPPER = BANK - LOWER
+SHARE = 128
+SHARE_LAST = 256
 WARM = 14
 RUN = 8
 
@@ -138,23 +138,30 @@ def tile_smcrossbaby_1_pb_t_kernel(
                     out=result[:, t, :], in_=acc[:], func=RELU, bias=w_bias[:, t : t + 1], scale=1.0
                 )
 
-        def first_words(g, u):
-            f_words = psum_first.tile([P, SIZES[g]], F32, tag="bank")
-            for c in range(SIZES[g] // P):
-                nc.tensor.transpose(
-                    f_words[:, c * P : (c + 1) * P],
-                    f_sb[g][:, c, :].bitcast(F32)[:, u * P : (u + 1) * P],
-                    ident[:],
-                )
-            first_banks[g, u] = f_words
+        def first_words(g, part):
+            us = (0, 1) if SIZES[g] < BANK else (part,)
+            f_words = psum_first.tile([P, len(us), SIZES[g]], F32, tag="bank")
+            for i, u in enumerate(us):
+                for c in range(SIZES[g] // P):
+                    nc.tensor.transpose(
+                        f_words[:, i, c * P : (c + 1) * P],
+                        f_sb[g][:, c, :].bitcast(F32)[:, u * P : (u + 1) * P],
+                        ident[:],
+                    )
+            first_banks[g, part] = f_words
 
-        def times_first(g, u):
-            if u == 0:
+        def parts(g):
+            return (0, 1) if SIZES[g] == BANK else (0,)
+
+        def times_first(g, part):
+            if part == 0:
                 product[g] = work.tile([P, PACK, SIZES[g]], F32, tag="product", name="product")
+            n = PACK // len(parts(g))
+            sl = slice(n * part, n * part + n)
             nc.vector.tensor_tensor(
-                out=product[g][:, 2 * u : 2 * u + 2, :],
-                in0=second[g][:, 2 * u : 2 * u + 2, :],
-                in1=first_banks[g, u][:].bitcast(BF16).rearrange("p (b e) -> p e b", e=2),
+                out=product[g][:, sl, :].rearrange("p (u e) b -> p u e b", e=2),
+                in0=second[g][:, sl, :].rearrange("p (u e) b -> p u e b", e=2),
+                in1=first_banks[g, part][:].rearrange("p u b -> p (u b)").bitcast(BF16).rearrange("p (u b e) -> p u e b", e=2, b=SIZES[g]),
                 op=MULT,
             )
 
@@ -266,114 +273,103 @@ def tile_smcrossbaby_1_pb_t_kernel(
         regroup_y(0, 0, by_vector)
         regroup_pair(psum_first, ws_grouped, 0, ws_sb[0], 0, by_scalar)
         quantise_y(0)
-        regroup_pair(psum_first, ws_grouped, 1, ws_sb[1], 0, by_vector)
+        regroup_pair(psum_first, ws_grouped, 1, ws_sb[1], 0, by_scalar)
         quantise(ws_q, ws_grouped, 0, 2 * P)
-        regroup_pair(psum_y, wi_grouped, 0, wi_sb[0], 0, by_scalar)
-        quantise(ws_q, ws_grouped, 2 * P, 2 * P)
         b_words = psum_head.tile([P, P], F32, tag="bank")
         nc.tensor.transpose(b_words[:], b_rows[:].bitcast(F32), ident[:])
         b_cols = keep.tile([P, 2 * PACK], BF16)
         nc.vector.tensor_copy(out=b_cols[:].bitcast(F32), in_=b_words[:, 0:PACK])
         bs_bf, bi_bf = b_cols[:, 0:PACK], b_cols[:, PACK : 2 * PACK]
+        regroup_pair(psum_y, wi_grouped, 0, wi_sb[0], 0, by_vector)
+        second_of(0, (0, 1))
+        quantise(ws_q, ws_grouped, 2 * P, 2 * P)
         regroup_pair(psum_y, wi_grouped, 1, wi_sb[1], 0, by_vector)
+        second_of(0, (2, 3))
         quantise(wi_q, wi_grouped, 0, 2 * P)
         quantise(wi_q, wi_grouped, 2 * P, 2 * P)
-        second_of(0, range(PACK))
+        regroup_y(1, 0, by_vector)
+        regroup_y(1, 1, by_scalar)
+        inter_of(0, (0, 1))
+        quantise_y(1)
+        first_words(0, 0)
+        inter_of(0, (2, 3))
+        times_first(0, 0)
         bout_bank = psum_head.tile([P, V], F32, tag="bank")
         nc.tensor.matmul(bout_bank[:], lhsT=ones[:], rhs=bout_row[:], start=True, stop=True)
         bout_bf = keep.tile([P, V], BF16)
         nc.vector.tensor_copy(out=bout_bf[:], in_=bout_bank[:])
-        regroup_y(1, 0, by_scalar)
-        regroup_y(1, 1, by_vector)
-        quantise_y(1)
-        first_words(0, 0)
-        first_words(0, 1)
-        times_first(0, 0)
-        times_first(0, 1)
-        inter_of(0, range(PACK))
 
         start_group(1)
+        z = new_z()
+        plus_inter(nc.gpsimd, 0, slice(SHARE, SIZES[0]), z[0][:, SHARE : SIZES[0], :])
         second_of(1, (0, 1))
         regroup_y(2, 0, by_vector)
-        second_of(1, (2, 3))
-        z = new_z()
-        plus_inter(nc.vector, 0, slice(0, SIZES[0]), z[0][:, 0 : SIZES[0], :])
-        quantise_z(z, 0, SIZES[0])
-        place(0, 0, z, 0, SIZES[0])
         first_words(1, 0)
+        second_of(1, (2, 3))
+        times_first(1, 0)
         wo_grouped, wo_q = new_grouped(V), new_quantised(V, "wo")
         regroup_pair(psum_head, wo_grouped, 0, wo_sb, 0, by_vector)
         regroup_y(2, 1, by_scalar)
-        inter_of(1, (0, 1))
         first_words(1, 1)
-        quantise_y(2)
-        inter_of(1, (2, 3))
-        quantise(wo_q, wo_grouped, 0, V)
-        times_first(1, 0)
-        head(0, 0, psum_head)
-        regroup_y(3, 0, by_scalar)
-        regroup_y(3, 1, by_scalar)
-
-        start_group(2)
-        second_of(2, (0, 1))
-        regroup_y(4, 0, by_scalar)
-        second_of(2, (2, 3))
-        late_words = y_words(4, 1)
+        inter_of(1, (0, 1))
         times_first(1, 1)
-        z = new_z()
-        plus_inter(nc.vector, 1, slice(0, LOWER), z[0][:, UPPER:BANK, :])
+        quantise_y(2)
+        regroup_y(3, 0, by_scalar)
+        inter_of(1, (2, 3))
+        regroup_y(3, 1, by_vector)
+        plus_inter(nc.vector, 0, slice(0, SHARE), z[0][:, 0:SHARE, :])
+        quantise(wo_q, wo_grouped, 0, V)
+        quantise_z(z, 0, SIZES[0])
+        place(0, 0, z, 0, SIZES[0])
         quantise_y(3)
-        inter_of(2, (0, 1))
         first_words(2, 0)
-        copy_pair(y_grouped[4], 1, late_words, by_vector)
-        quantise_z(z, UPPER, LOWER)
-        place(1, 0, z, UPPER, LOWER)
-        quantise_y(4)
-        inter_of(2, (2, 3))
-        first_words(2, 1)
 
-        for r in range(3, N_GROUPS):
+        for r in range(2, N_GROUPS):
             start_group(r)
             second_of(r, (0, 1))
+            if SIZES[r] == BANK:
+                first_words(r, 1)
             z = new_z()
-            plus_inter(nc.gpsimd, r - 2, slice(LOWER, BANK), z[0][:, 0:UPPER, :])
-            times_first(r - 1, 0)
-            if r + 2 < N_GROUPS and r > 3:
-                head(r - 2, 0, psum_head)
+            n = SIZES[r - 1]
+            share = SHARE if r < N_GROUPS - 1 else SHARE_LAST
+            plus_inter(nc.gpsimd, r - 1, slice(share, n), z[0][:, share:n, :])
+            if SIZES[r] == BANK:
+                times_first(r, 0)
             if r + 2 < N_GROUPS:
                 regroup_y(r + 2, 0, by_scalar)
             second_of(r, (2, 3))
-            times_first(r - 1, 1)
-            if r == 3:
-                head(1, 0, psum_head)
-            if r > 3:
-                head(r - 3, 1, psum_head)
-            if r + 2 < N_GROUPS and SIZES[r + 2] == BANK:
-                regroup_y(r + 2, 1, by_scalar)
+            pair_one = r + 2 < N_GROUPS and SIZES[r + 2] == BANK
+            late = pair_one and r % 2 == 0
+            if pair_one:
+                words = y_words(r + 2, 1)
+                if not late:
+                    copy_pair(y_grouped[r + 2], 1, words, by_scalar)
+            if SIZES[r] < BANK:
+                times_first(r, 0)
+            head(r - 2, 0, psum_head)
+            if SIZES[r] == BANK:
+                times_first(r, 1)
+            if late:
+                copy_pair(y_grouped[r + 2], 1, words, by_vector)
             inter_of(r, (0, 1))
-            first_words(r, 0)
-            plus_inter(nc.vector, r - 1, slice(0, LOWER), z[0][:, UPPER:BANK, :])
+            if SIZES[r - 2] == BANK:
+                head(r - 2, 1, psum_y)
+            inter_of(r, (2, 3))
+            if r + 1 < N_GROUPS:
+                first_words(r + 1, 0)
+            plus_inter(nc.vector, r - 1, slice(0, share), z[0][:, 0:share, :])
             if r + 2 < N_GROUPS:
                 quantise_y(r + 2)
-            else:
-                head(r - 2, 0, psum_head)
-            quantise_z(z, 0, BANK)
-            place(r - 2, LOWER // P, z, 0, UPPER)
-            place(r - 1, 0, z, UPPER, LOWER)
-            inter_of(r, (2, 3))
-            first_words(r, 1)
+            quantise_z(z, 0, n)
+            place(r - 1, 0, z, 0, n)
 
         last = N_GROUPS - 1
         z = new_z()
-        plus_inter(nc.gpsimd, last - 1, slice(LOWER, BANK), z[0][:, 0:UPPER, :])
-        place(last - 1, LOWER // P, z, 0, UPPER)
-        times_first(last, 0)
-        times_first(last, 1)
+        n = SIZES[last]
+        plus_inter(nc.vector, last, slice(0, n), z[0][:, 0:n, :])
         head(last - 1, 0, psum_head)
-        head(last - 2, 1, psum_y)
-        plus_inter(nc.vector, last, slice(0, SIZES[last]), z[0][:, UPPER:BANK, :])
-        quantise_z(z, 0, UPPER)
-        quantise_z(z, UPPER, SIZES[last])
-        place(last, 0, z, UPPER, SIZES[last])
-        head(last - 1, 1, psum_head)
+        quantise_z(z, 0, n)
+        place(last, 0, z, 0, n)
+        if SIZES[last - 1] == BANK:
+            head(last - 1, 1, psum_y)
         last_head(last)

@@ -22,7 +22,8 @@ STARTS = tuple(sum(SIZES[:g]) for g in range(N_GROUPS))
 BANK = 512
 SHARE = 128
 SHARE_LAST = 256
-WARM = 14
+WARM = 22
+STAY_WARM = 4
 RUN = 8
 
 FLOPS = 2 * BATCH * K * (K + K + V)
@@ -57,8 +58,12 @@ def tile_smcrossbaby_1_pb_t_kernel(
         ones = keep.tile([P, P], BF16)
         nc.vector.memset(ones[:], 1.0)
         warm = psum_acc.tile([P, P], F32, tag="acc")
-        for i in range(WARM):
-            nc.tensor.matmul(warm[:], lhsT=ones[:], rhs=ones[:], start=True, stop=True)
+
+        def keep_warm(n):
+            for i in range(n):
+                nc.tensor.matmul(warm[:], lhsT=ones[:], rhs=ones[:], start=True, stop=True)
+
+        keep_warm(WARM)
         nc.vector.memset(b_rows[:], 0.0)
         nc.vector.memset(bout_row[:], 0.0)
 
@@ -271,8 +276,10 @@ def tile_smcrossbaby_1_pb_t_kernel(
         wi_q = new_quantised(K, "wi")
         start_group(0)
         regroup_y(0, 0, by_vector)
+        keep_warm(STAY_WARM)
         regroup_pair(psum_first, ws_grouped, 0, ws_sb[0], 0, by_scalar)
         quantise_y(0)
+        keep_warm(STAY_WARM)
         regroup_pair(psum_first, ws_grouped, 1, ws_sb[1], 0, by_scalar)
         quantise(ws_q, ws_grouped, 0, 2 * P)
         b_words = psum_head.tile([P, P], F32, tag="bank")
@@ -280,6 +287,7 @@ def tile_smcrossbaby_1_pb_t_kernel(
         b_cols = keep.tile([P, 2 * PACK], BF16)
         nc.vector.tensor_copy(out=b_cols[:].bitcast(F32), in_=b_words[:, 0:PACK])
         bs_bf, bi_bf = b_cols[:, 0:PACK], b_cols[:, PACK : 2 * PACK]
+        keep_warm(STAY_WARM)
         regroup_pair(psum_y, wi_grouped, 0, wi_sb[0], 0, by_vector)
         second_of(0, (0, 1))
         quantise(ws_q, ws_grouped, 2 * P, 2 * P)

@@ -20,8 +20,8 @@ SIZES = (256, 512, 512, 512, 512, 512, 512, 512, 256)
 N_GROUPS = len(SIZES)
 STARTS = tuple(sum(SIZES[:g]) for g in range(N_GROUPS))
 BANK = 512
-SHARE = 128
-SHARE_LAST = 256
+SHARE = 176
+SHARE_LAST = 320
 WARM = 22
 STAY_WARM = 4
 RUN = 8
@@ -72,6 +72,14 @@ def tile_smcrossbaby_1_pb_t_kernel(
                 out=w_sb[u][:], in_=w[256 * u : 256 * u + 256, :].rearrange("(p e) k -> p e k", e=2)
             )
 
+        def load_weight_chunk(w_sb, w, u, e):
+            nc.sync.dma_start(
+                out=w_sb[u][:, e, :], in_=w[256 * u : 256 * u + 256, :].rearrange("(p e) k -> p e k", e=2)[:, e, :]
+            )
+
+        def load_y_chunk(g, j):
+            nc.sync.dma_start(out=y_sb[g][:, j, :], in_=group_rows(y2, g)[:, j, :])
+
         def load_y(g):
             nc.sync.dma_start(out=y_sb[g][:], in_=group_rows(y2, g))
 
@@ -108,6 +116,17 @@ def tile_smcrossbaby_1_pb_t_kernel(
             grouped_words = grouped[:].bitcast(F32).rearrange("p (c u) -> p c u", u=2)
             copy_out(
                 out=grouped_words[:, pair * 2 * P : (pair + 1) * 2 * P, :],
+                in_=words[:].rearrange("p u c -> p c u"),
+            )
+
+        def regroup_chunk(bank_pool, grouped, chunk, rows_sb, index, copy_out):
+            words = bank_pool.tile([P, 2, P], F32, tag="bank")
+            for u in range(2):
+                nc.tensor.transpose(
+                    words[:, u, :], rows_sb[:, index, :].bitcast(F32)[:, u * P : (u + 1) * P], ident[:]
+                )
+            copy_out(
+                out=grouped[:].bitcast(F32).rearrange("p (c u) -> p c u", u=2)[:, chunk * P : (chunk + 1) * P, :],
                 in_=words[:].rearrange("p u c -> p c u"),
             )
 
@@ -288,7 +307,7 @@ def tile_smcrossbaby_1_pb_t_kernel(
         nc.vector.tensor_copy(out=b_cols[:].bitcast(F32), in_=b_words[:, 0:PACK])
         bs_bf, bi_bf = b_cols[:, 0:PACK], b_cols[:, PACK : 2 * PACK]
         keep_warm(STAY_WARM)
-        regroup_pair(psum_y, wi_grouped, 0, wi_sb[0], 0, by_vector)
+        regroup_pair(psum_y, wi_grouped, 0, wi_sb[0], 0, by_scalar)
         second_of(0, (0, 1))
         quantise(ws_q, ws_grouped, 2 * P, 2 * P)
         regroup_pair(psum_y, wi_grouped, 1, wi_sb[1], 0, by_vector)
@@ -322,7 +341,7 @@ def tile_smcrossbaby_1_pb_t_kernel(
         inter_of(1, (0, 1))
         times_first(1, 1)
         quantise_y(2)
-        regroup_y(3, 0, by_scalar)
+        regroup_y(3, 0, by_vector)
         inter_of(1, (2, 3))
         regroup_y(3, 1, by_vector)
         plus_inter(nc.vector, 0, slice(0, SHARE), z[0][:, 0:SHARE, :])
@@ -347,7 +366,7 @@ def tile_smcrossbaby_1_pb_t_kernel(
                 regroup_y(r + 2, 0, by_scalar)
             second_of(r, (2, 3))
             pair_one = r + 2 < N_GROUPS and SIZES[r + 2] == BANK
-            late = pair_one and r % 2 == 0
+            late = pair_one and r in (2,)
             if pair_one:
                 words = y_words(r + 2, 1)
                 if not late:

@@ -147,20 +147,23 @@ def tile_smcrossbaby_1_pb_t_kernel(
             )
 
         def relu_of_product(g, w_q, w_bias, result, ts):
-            for t in ts:
-                acc = psum_acc.tile([P, SIZES[g]], F32, tag="acc")
-                nc.tensor.matmul_mx(
-                    out=acc[:],
-                    lhsT=w_q[0][:, t * P : (t + 1) * P].bitcast(FP8X4),
-                    lhsT_scale=w_q[1][:, t * P : (t + 1) * P],
-                    rhs=y_q[g][0][:].bitcast(FP8X4),
-                    rhs_scale=y_q[g][1][:],
-                    start=True,
-                    stop=True,
-                )
-                nc.scalar.activation(
-                    out=result[:, t, :], in_=acc[:], func=RELU, bias=w_bias[:, t : t + 1], scale=1.0
-                )
+            per_bank = BANK // SIZES[g]
+            for t0 in ts[::per_bank]:
+                acc = psum_acc.tile([P, per_bank, SIZES[g]], F32, tag="acc")
+                for i in range(per_bank):
+                    nc.tensor.matmul_mx(
+                        out=acc[:, i, :],
+                        lhsT=w_q[0][:, (t0 + i) * P : (t0 + i + 1) * P].bitcast(FP8X4),
+                        lhsT_scale=w_q[1][:, (t0 + i) * P : (t0 + i + 1) * P],
+                        rhs=y_q[g][0][:].bitcast(FP8X4),
+                        rhs_scale=y_q[g][1][:],
+                        start=True,
+                        stop=True,
+                    )
+                for i in range(per_bank):
+                    nc.scalar.activation(
+                        out=result[:, t0 + i, :], in_=acc[:, i, :], func=RELU, bias=w_bias[:, t0 + i : t0 + i + 1], scale=1.0
+                    )
 
         def first_words(g, part):
             us = (0, 1) if SIZES[g] < BANK else (part,)
@@ -308,23 +311,20 @@ def tile_smcrossbaby_1_pb_t_kernel(
         bs_bf, bi_bf = b_cols[:, 0:PACK], b_cols[:, PACK : 2 * PACK]
         keep_warm(STAY_WARM)
         regroup_pair(psum_y, wi_grouped, 0, wi_sb[0], 0, by_scalar)
-        second_of(0, (0, 1))
         quantise(ws_q, ws_grouped, 2 * P, 2 * P)
         regroup_pair(psum_y, wi_grouped, 1, wi_sb[1], 0, by_vector)
-        second_of(0, (2, 3))
-        quantise(wi_q, wi_grouped, 0, 2 * P)
-        quantise(wi_q, wi_grouped, 2 * P, 2 * P)
+        second_of(0, range(PACK))
+        quantise(wi_q, wi_grouped, 0, K)
         regroup_y(1, 0, by_vector)
         regroup_y(1, 1, by_scalar)
-        inter_of(0, (0, 1))
         quantise_y(1)
         first_words(0, 0)
-        inter_of(0, (2, 3))
+        inter_of(0, range(PACK))
         times_first(0, 0)
         bout_bank = psum_head.tile([P, V], F32, tag="bank")
         nc.tensor.matmul(bout_bank[:], lhsT=ones[:], rhs=bout_row[:], start=True, stop=True)
         bout_bf = keep.tile([P, V], BF16)
-        nc.vector.tensor_copy(out=bout_bf[:], in_=bout_bank[:])
+        nc.scalar.copy(out=bout_bf[:], in_=bout_bank[:])
 
         start_group(1)
         z = new_z()

@@ -9,6 +9,7 @@ U32 = mybir.dt.uint32
 U8 = mybir.dt.uint8
 FP8X4 = mybir.dt.float8_e4m3fn_x4
 RELU = mybir.ActivationFunctionType.Relu
+IDENTITY = mybir.ActivationFunctionType.Identity
 MULT = mybir.AluOpType.mult
 ADD = mybir.AluOpType.add
 
@@ -21,7 +22,7 @@ N_GROUPS = len(SIZES)
 STARTS = tuple(sum(SIZES[:g]) for g in range(N_GROUPS))
 BANK = 512
 SHARE = 176
-SHARE_LAST = 320
+SHARE_LAST = 448
 WARM = 22
 STAY_WARM = 4
 RUN = 8
@@ -44,6 +45,8 @@ def tile_smcrossbaby_1_pb_t_kernel(
 
         ident = keep.tile([P, P], F32)
         make_identity(nc, ident[:])
+        ident_bf = keep.tile([P, P], BF16)
+        make_identity(nc, ident_bf[:])
 
         def group_rows(dram, g):
             return dram[STARTS[g] : STARTS[g] + SIZES[g], :].rearrange("(p j) k -> p j k", j=SIZES[g] // P)
@@ -55,6 +58,9 @@ def tile_smcrossbaby_1_pb_t_kernel(
         wo_sb = keep.tile([P, V // P, K], BF16)
         b_rows = keep.tile([P, 2 * P], BF16)
         bout_row = keep.tile([P, V], BF16)
+        bo_rows = keep.tile([P, P], BF16)
+        bo_cols = keep.tile([P, V // P], F32)
+        out_t = keep.tile([P, V // P, BANK], F32)
         ones = keep.tile([P, P], BF16)
         nc.vector.memset(ones[:], 1.0)
         warm = psum_acc.tile([P, P], F32, tag="acc")
@@ -66,6 +72,7 @@ def tile_smcrossbaby_1_pb_t_kernel(
         keep_warm(WARM)
         nc.vector.memset(b_rows[:], 0.0)
         nc.vector.memset(bout_row[:], 0.0)
+        nc.vector.memset(bo_rows[:], 0.0)
 
         def load_weight(w_sb, w, u):
             nc.sync.dma_start(
@@ -96,6 +103,7 @@ def tile_smcrossbaby_1_pb_t_kernel(
         load_weight(wi_sb, w_int, 1)
         load_y(1)
         load_f(0)
+        nc.sync.dma_start(out=bo_rows[0 : V // P, :], in_=b_out.rearrange("(c p) -> c p", p=P))
         load_y(2)
         nc.sync.dma_start(out=wo_sb[:], in_=w_out.rearrange("(c p) m -> p c m", p=P))
         load_f(1)
@@ -236,6 +244,37 @@ def tile_smcrossbaby_1_pb_t_kernel(
             )
             nc.sync.dma_start(out=group_rows(out, g)[:, 2 * h : 2 * h + 2, :], in_=out_sb[:])
 
+        def head_products_by_scalar(g):
+            for c in range(V // P):
+                bank = psum_y.tile([P, BANK], F32, tag="bank")
+                codes, scales = z_place[g, 0][0:2]
+                nc.tensor.matmul_mx(
+                    out=bank[:],
+                    lhsT=wo_q[0][:, c * P : (c + 1) * P].bitcast(FP8X4),
+                    lhsT_scale=wo_q[1][:, c * P : (c + 1) * P],
+                    rhs=codes[:, 0:BANK].bitcast(FP8X4),
+                    rhs_scale=scales[:, 0:BANK],
+                    start=True,
+                    stop=True,
+                )
+                nc.scalar.activation(
+                    out=out_t[:, c, :], in_=bank[:], func=IDENTITY, bias=bo_cols[:, c : c + 1], scale=1.0
+                )
+
+        def head_back_by_scalar(g):
+            for h, pool in ((0, psum_y), (1, psum_y)):
+                bank = pool.tile([P, 2, V], F32, tag="bank")
+                for j in range(2):
+                    for c in range(V // P):
+                        nc.tensor.transpose(
+                            bank[:, j, c * P : (c + 1) * P],
+                            out_t[:, c, (2 * h + j) * P : (2 * h + j + 1) * P],
+                            ident[:],
+                        )
+                out_sb = work.tile([P, 2, V], F32, bufs=4, tag="out")
+                nc.scalar.copy(out=out_sb[:], in_=bank[:])
+                nc.sync.dma_start(out=group_rows(out, g)[:, 2 * h : 2 * h + 2, :], in_=out_sb[:])
+
         def last_head(g):
             for c, pool in ((0, psum_y), (1, psum_first)):
                 bank = pool.tile([P, V], F32, tag="bank")
@@ -324,11 +363,11 @@ def tile_smcrossbaby_1_pb_t_kernel(
         bout_bank = psum_head.tile([P, V], F32, tag="bank")
         nc.tensor.matmul(bout_bank[:], lhsT=ones[:], rhs=bout_row[:], start=True, stop=True)
         bout_bf = keep.tile([P, V], BF16)
-        nc.scalar.copy(out=bout_bf[:], in_=bout_bank[:])
+        nc.vector.tensor_copy(out=bout_bf[:], in_=bout_bank[:])
 
         start_group(1)
         z = new_z()
-        plus_inter(nc.gpsimd, 0, slice(SHARE, SIZES[0]), z[0][:, SHARE : SIZES[0], :])
+        plus_inter(nc.gpsimd, 0, slice(0, SIZES[0]), z[0][:, 0 : SIZES[0], :])
         second_of(1, (0, 1))
         regroup_y(2, 0, by_vector)
         first_words(1, 0)
@@ -344,12 +383,15 @@ def tile_smcrossbaby_1_pb_t_kernel(
         regroup_y(3, 0, by_vector)
         inter_of(1, (2, 3))
         regroup_y(3, 1, by_vector)
-        plus_inter(nc.vector, 0, slice(0, SHARE), z[0][:, 0:SHARE, :])
         quantise(wo_q, wo_grouped, 0, V)
         quantise_z(z, 0, SIZES[0])
         place(0, 0, z, 0, SIZES[0])
         quantise_y(3)
         first_words(2, 0)
+
+        bo_bank = psum_head.tile([P, P], F32, tag="bank")
+        nc.tensor.matmul(bo_bank[:], lhsT=bo_rows[:], rhs=ident_bf[:], start=True, stop=True)
+        nc.scalar.copy(out=bo_cols[:], in_=bo_bank[:, 0 : V // P])
 
         for r in range(2, N_GROUPS):
             start_group(r)
@@ -373,15 +415,18 @@ def tile_smcrossbaby_1_pb_t_kernel(
                     copy_pair(y_grouped[r + 2], 1, words, by_scalar)
             if SIZES[r] < BANK:
                 times_first(r, 0)
-            head(r - 2, 0, psum_head)
+            if r < N_GROUPS - 1:
+                head(r - 2, 0, psum_head)
             if SIZES[r] == BANK:
                 times_first(r, 1)
             if late:
                 copy_pair(y_grouped[r + 2], 1, words, by_vector)
             inter_of(r, (0, 1))
-            if SIZES[r - 2] == BANK:
+            if SIZES[r - 2] == BANK and r < N_GROUPS - 1:
                 head(r - 2, 1, psum_y)
             inter_of(r, (2, 3))
+            if r == N_GROUPS - 1:
+                head_products_by_scalar(r - 2)
             if r + 1 < N_GROUPS:
                 first_words(r + 1, 0)
             plus_inter(nc.vector, r - 1, slice(0, share), z[0][:, 0:share, :])
@@ -393,6 +438,7 @@ def tile_smcrossbaby_1_pb_t_kernel(
         last = N_GROUPS - 1
         z = new_z()
         n = SIZES[last]
+        head_back_by_scalar(last - 2)
         plus_inter(nc.vector, last, slice(0, n), z[0][:, 0:n, :])
         head(last - 1, 0, psum_head)
         quantise_z(z, 0, n)

@@ -95,15 +95,15 @@ def tile_smcrossbaby_1_pb_t_kernel(
 
         load_y(0)
         load_weight(ws_sb, w_second, 0)
-        nc.sync.dma_start(out=b_rows[0:2, :], in_=b_second.rearrange("(u k) -> u k", u=2))
-        nc.sync.dma_start(out=b_rows[2:4, :], in_=b_int.rearrange("(u k) -> u k", u=2))
-        nc.sync.dma_start(out=bout_row[0:1, :], in_=b_out.rearrange("(o v) -> o v", o=1))
+        nc.scalar.dma_start(out=b_rows[0:2, :], in_=b_second.rearrange("(u k) -> u k", u=2))
+        nc.scalar.dma_start(out=b_rows[2:4, :], in_=b_int.rearrange("(u k) -> u k", u=2))
+        nc.scalar.dma_start(out=bout_row[0:1, :], in_=b_out.rearrange("(o v) -> o v", o=1))
         load_weight(ws_sb, w_second, 1)
         load_weight(wi_sb, w_int, 0)
         load_weight(wi_sb, w_int, 1)
         load_y(1)
         load_f(0)
-        nc.sync.dma_start(out=bo_rows[0 : V // P, :], in_=b_out.rearrange("(c p) -> c p", p=P))
+        nc.scalar.dma_start(out=bo_rows[0 : V // P, :], in_=b_out.rearrange("(c p) -> c p", p=P))
         load_y(2)
         nc.sync.dma_start(out=wo_sb[:], in_=w_out.rearrange("(c p) m -> p c m", p=P))
         load_f(1)

@@ -40,8 +40,7 @@ def tile_smcrossbaby_1_pb_t_kernel(
         work = ctx.enter_context(tc.tile_pool(name="work", bufs=2))
         psum_y = ctx.enter_context(tc.psum_pool(name="psum_y", bufs=2))
         psum_first = ctx.enter_context(tc.psum_pool(name="psum_first", bufs=2))
-        psum_acc = ctx.enter_context(tc.psum_pool(name="psum_acc", bufs=3))
-        psum_head = ctx.enter_context(tc.psum_pool(name="psum_head", bufs=1))
+        psum_acc = ctx.enter_context(tc.psum_pool(name="psum_acc", bufs=4))
 
         ident = keep.tile([P, P], F32)
         make_identity(nc, ident[:])
@@ -343,7 +342,7 @@ def tile_smcrossbaby_1_pb_t_kernel(
         keep_warm(STAY_WARM)
         regroup_pair(psum_first, ws_grouped, 1, ws_sb[1], 0, by_scalar)
         quantise(ws_q, ws_grouped, 0, 2 * P)
-        b_words = psum_head.tile([P, P], F32, tag="bank")
+        b_words = psum_acc.tile([P, P], F32, tag="acc")
         nc.tensor.transpose(b_words[:], b_rows[:].bitcast(F32), ident[:])
         b_cols = keep.tile([P, 2 * PACK], BF16)
         nc.vector.tensor_copy(out=b_cols[:].bitcast(F32), in_=b_words[:, 0:PACK])
@@ -360,7 +359,7 @@ def tile_smcrossbaby_1_pb_t_kernel(
         first_words(0, 0)
         inter_of(0, range(PACK))
         times_first(0, 0)
-        bout_bank = psum_head.tile([P, V], F32, tag="bank")
+        bout_bank = psum_acc.tile([P, V], F32, tag="acc")
         nc.tensor.matmul(bout_bank[:], lhsT=ones[:], rhs=bout_row[:], start=True, stop=True)
         bout_bf = keep.tile([P, V], BF16)
         nc.vector.tensor_copy(out=bout_bf[:], in_=bout_bank[:])
@@ -374,7 +373,7 @@ def tile_smcrossbaby_1_pb_t_kernel(
         second_of(1, (2, 3))
         times_first(1, 0)
         wo_grouped, wo_q = new_grouped(V), new_quantised(V, "wo")
-        regroup_pair(psum_head, wo_grouped, 0, wo_sb, 0, by_vector)
+        regroup_pair(psum_y, wo_grouped, 0, wo_sb, 0, by_vector)
         regroup_y(2, 1, by_scalar)
         first_words(1, 1)
         inter_of(1, (0, 1))
@@ -389,42 +388,31 @@ def tile_smcrossbaby_1_pb_t_kernel(
         quantise_y(3)
         first_words(2, 0)
 
-        bo_bank = psum_head.tile([P, P], F32, tag="bank")
+        bo_bank = psum_acc.tile([P, P], F32, tag="acc")
         nc.tensor.matmul(bo_bank[:], lhsT=bo_rows[:], rhs=ident_bf[:], start=True, stop=True)
         nc.scalar.copy(out=bo_cols[:], in_=bo_bank[:, 0 : V // P])
 
         for r in range(2, N_GROUPS):
             start_group(r)
-            second_of(r, (0, 1))
+            second_of(r, range(PACK))
             if SIZES[r] == BANK:
                 first_words(r, 1)
             z = new_z()
             n = SIZES[r - 1]
             share = SHARE if r < N_GROUPS - 1 else SHARE_LAST
             plus_inter(nc.gpsimd, r - 1, slice(share, n), z[0][:, share:n, :])
-            if SIZES[r] == BANK:
-                times_first(r, 0)
+            for part in parts(r):
+                times_first(r, part)
             if r + 2 < N_GROUPS:
                 regroup_y(r + 2, 0, by_scalar)
-            second_of(r, (2, 3))
-            pair_one = r + 2 < N_GROUPS and SIZES[r + 2] == BANK
-            late = pair_one and r in (2,)
-            if pair_one:
-                words = y_words(r + 2, 1)
-                if not late:
-                    copy_pair(y_grouped[r + 2], 1, words, by_scalar)
-            if SIZES[r] < BANK:
-                times_first(r, 0)
-            if r < N_GROUPS - 1:
-                head(r - 2, 0, psum_head)
-            if SIZES[r] == BANK:
-                times_first(r, 1)
-            if late:
-                copy_pair(y_grouped[r + 2], 1, words, by_vector)
+            if r + 2 < N_GROUPS and SIZES[r + 2] == BANK:
+                regroup_y(r + 2, 1, by_vector if r == 2 else by_scalar)
             inter_of(r, (0, 1))
+            if r < N_GROUPS - 1:
+                head(r - 2, 0, psum_y)
+            inter_of(r, (2, 3))
             if SIZES[r - 2] == BANK and r < N_GROUPS - 1:
                 head(r - 2, 1, psum_y)
-            inter_of(r, (2, 3))
             if r == N_GROUPS - 1:
                 head_products_by_scalar(r - 2)
             if r + 1 < N_GROUPS:
@@ -440,7 +428,7 @@ def tile_smcrossbaby_1_pb_t_kernel(
         n = SIZES[last]
         head_back_by_scalar(last - 2)
         plus_inter(nc.vector, last, slice(0, n), z[0][:, 0:n, :])
-        head(last - 1, 0, psum_head)
+        head(last - 1, 0, psum_y)
         quantise_z(z, 0, n)
         place(last, 0, z, 0, n)
         if SIZES[last - 1] == BANK:

from contextlib import ExitStack

import concourse.mybir as mybir
from concourse.masks import make_identity

F32 = mybir.dt.float32
BF16 = mybir.dt.bfloat16
U32 = mybir.dt.uint32
U8 = mybir.dt.uint8
FP8X4 = mybir.dt.float8_e4m3fn_x4
RELU = mybir.ActivationFunctionType.Relu
IDENTITY = mybir.ActivationFunctionType.Identity
MULT = mybir.AluOpType.mult
ADD = mybir.AluOpType.add

P = 128
PACK = 4
K = P * PACK
BATCH, V = 4096, 256
SIZES = (256, 512, 512, 512, 512, 512, 512, 512, 256)
N_GROUPS = len(SIZES)
STARTS = tuple(sum(SIZES[:g]) for g in range(N_GROUPS))
BANK = 512
SHARE = 176
SHARE_LAST = 448
WARM = 22
STAY_WARM = 4
RUN = 8

FLOPS = 2 * BATCH * K * (K + K + V)


def tile_smcrossbaby_1_pb_t_kernel(
    tc, y2, first, w_second, b_second, w_int, b_int, w_out, b_out, out
):
    nc = tc.nc
    with ExitStack() as ctx:
        ctx.enter_context(tc.manual_schedule())
        keep = ctx.enter_context(tc.tile_pool(name="keep", bufs=1))
        work = ctx.enter_context(tc.tile_pool(name="work", bufs=2))
        psum_y = ctx.enter_context(tc.psum_pool(name="psum_y", bufs=2))
        psum_first = ctx.enter_context(tc.psum_pool(name="psum_first", bufs=2))
        psum_acc = ctx.enter_context(tc.psum_pool(name="psum_acc", bufs=4))

        ident = keep.tile([P, P], F32)
        make_identity(nc, ident[:])
        ident_bf = keep.tile([P, P], BF16)
        make_identity(nc, ident_bf[:])

        def group_rows(dram, g):
            return dram[STARTS[g] : STARTS[g] + SIZES[g], :].rearrange("(p j) k -> p j k", j=SIZES[g] // P)

        y_sb = [keep.tile([P, SIZES[g] // P, K], BF16, name="y_sb%d" % g) for g in range(N_GROUPS)]
        f_sb = [keep.tile([P, SIZES[g] // P, K], BF16, name="f_sb%d" % g) for g in range(N_GROUPS)]
        ws_sb = [keep.tile([P, 2, K], BF16, name="ws_sb%d" % u) for u in range(2)]
        wi_sb = [keep.tile([P, 2, K], BF16, name="wi_sb%d" % u) for u in range(2)]
        wo_sb = keep.tile([P, V // P, K], BF16)
        b_rows = keep.tile([P, 2 * P], BF16)
        bout_row = keep.tile([P, V], BF16)
        bo_rows = keep.tile([P, P], BF16)
        bo_cols = keep.tile([P, V // P], F32)
        out_t = keep.tile([P, V // P, BANK], F32)
        ones = keep.tile([P, P], BF16)
        nc.vector.memset(ones[:], 1.0)
        warm = psum_acc.tile([P, P], F32, tag="acc")

        def keep_warm(n):
            for i in range(n):
                nc.tensor.matmul(warm[:], lhsT=ones[:], rhs=ones[:], start=True, stop=True)

        keep_warm(WARM)
        nc.vector.memset(b_rows[:], 0.0)
        nc.vector.memset(bout_row[:], 0.0)
        nc.vector.memset(bo_rows[:], 0.0)

        def load_weight(w_sb, w, u):
            nc.sync.dma_start(
                out=w_sb[u][:], in_=w[256 * u : 256 * u + 256, :].rearrange("(p e) k -> p e k", e=2)
            )

        def load_weight_chunk(w_sb, w, u, e):
            nc.sync.dma_start(
                out=w_sb[u][:, e, :], in_=w[256 * u : 256 * u + 256, :].rearrange("(p e) k -> p e k", e=2)[:, e, :]
            )

        def load_y_chunk(g, j):
            nc.sync.dma_start(out=y_sb[g][:, j, :], in_=group_rows(y2, g)[:, j, :])

        def load_y(g):
            nc.sync.dma_start(out=y_sb[g][:], in_=group_rows(y2, g))

        def load_f(g):
            nc.sync.dma_start(out=f_sb[g][:], in_=group_rows(first, g))

        load_y(0)
        load_weight(ws_sb, w_second, 0)
        nc.scalar.dma_start(out=b_rows[0:2, :], in_=b_second.rearrange("(u k) -> u k", u=2))
        nc.scalar.dma_start(out=b_rows[2:4, :], in_=b_int.rearrange("(u k) -> u k", u=2))
        nc.scalar.dma_start(out=bout_row[0:1, :], in_=b_out.rearrange("(o v) -> o v", o=1))
        load_weight(ws_sb, w_second, 1)
        load_weight(wi_sb, w_int, 0)
        load_weight(wi_sb, w_int, 1)
        load_y(1)
        load_f(0)
        nc.scalar.dma_start(out=bo_rows[0 : V // P, :], in_=b_out.rearrange("(c p) -> c p", p=P))
        load_y(2)
        nc.sync.dma_start(out=wo_sb[:], in_=w_out.rearrange("(c p) m -> p c m", p=P))
        load_f(1)
        for g in range(2, N_GROUPS):
            load_f(g)
            if g + 1 < N_GROUPS:
                load_y(g + 1)

        def regroup_pair(bank_pool, grouped, pair, rows_sb, chunk, copy_out):
            words = bank_pool.tile([P, 2, 2 * P], F32, tag="bank")
            for c in range(2):
                for u in range(2):
                    nc.tensor.transpose(
                        words[:, u, c * P : (c + 1) * P],
                        rows_sb[:, chunk + c, :].bitcast(F32)[:, u * P : (u + 1) * P],
                        ident[:],
                    )
            grouped_words = grouped[:].bitcast(F32).rearrange("p (c u) -> p c u", u=2)
            copy_out(
                out=grouped_words[:, pair * 2 * P : (pair + 1) * 2 * P, :],
                in_=words[:].rearrange("p u c -> p c u"),
            )

        def regroup_chunk(bank_pool, grouped, chunk, rows_sb, index, copy_out):
            words = bank_pool.tile([P, 2, P], F32, tag="bank")
            for u in range(2):
                nc.tensor.transpose(
                    words[:, u, :], rows_sb[:, index, :].bitcast(F32)[:, u * P : (u + 1) * P], ident[:]
                )
            copy_out(
                out=grouped[:].bitcast(F32).rearrange("p (c u) -> p c u", u=2)[:, chunk * P : (chunk + 1) * P, :],
                in_=words[:].rearrange("p u c -> p c u"),
            )

        def new_grouped(rows):
            grouped = work.tile([P, rows * PACK], BF16, align_bytes=64, tag="grouped", bufs=3)
            return grouped

        def new_quantised(cols, name):
            codes = keep.tile([P, cols], U32, align_bytes=64, name=name + "_codes")
            scales = keep.tile([P, cols], U8, align_bytes=64, name=name + "_scales")
            return codes, scales

        def quantise(q, grouped, start, cols):
            nc.vector.quantize_mx(
                out=q[0][:, start : start + cols].bitcast(FP8X4),
                scales=q[1][:, start : start + cols],
                in_=grouped[:, PACK * start : PACK * (start + cols)],
            )

        def relu_of_product(g, w_q, w_bias, result, ts):
            per_bank = BANK // SIZES[g]
            for t0 in ts[::per_bank]:
                acc = psum_acc.tile([P, per_bank, SIZES[g]], F32, tag="acc")
                for i in range(per_bank):
                    nc.tensor.matmul_mx(
                        out=acc[:, i, :],
                        lhsT=w_q[0][:, (t0 + i) * P : (t0 + i + 1) * P].bitcast(FP8X4),
                        lhsT_scale=w_q[1][:, (t0 + i) * P : (t0 + i + 1) * P],
                        rhs=y_q[g][0][:].bitcast(FP8X4),
                        rhs_scale=y_q[g][1][:],
                        start=True,
                        stop=True,
                    )
                for i in range(per_bank):
                    nc.scalar.activation(
                        out=result[:, t0 + i, :], in_=acc[:, i, :], func=RELU, bias=w_bias[:, t0 + i : t0 + i + 1], scale=1.0
                    )

        def first_words(g, part):
            us = (0, 1) if SIZES[g] < BANK else (part,)
            f_words = psum_first.tile([P, len(us), SIZES[g]], F32, tag="bank")
            for i, u in enumerate(us):
                for c in range(SIZES[g] // P):
                    nc.tensor.transpose(
                        f_words[:, i, c * P : (c + 1) * P],
                        f_sb[g][:, c, :].bitcast(F32)[:, u * P : (u + 1) * P],
                        ident[:],
                    )
            first_banks[g, part] = f_words

        def parts(g):
            return (0, 1) if SIZES[g] == BANK else (0,)

        def times_first(g, part):
            if part == 0:
                product[g] = work.tile([P, PACK, SIZES[g]], F32, tag="product", name="product")
            n = PACK // len(parts(g))
            sl = slice(n * part, n * part + n)
            nc.vector.tensor_tensor(
                out=product[g][:, sl, :].rearrange("p (u e) b -> p u e b", e=2),
                in0=second[g][:, sl, :].rearrange("p (u e) b -> p u e b", e=2),
                in1=first_banks[g, part][:].rearrange("p u b -> p (u b)").bitcast(BF16).rearrange("p (u b e) -> p u e b", e=2, b=SIZES[g]),
                op=MULT,
            )

        def plus_inter(engine, g, cols, z_part):
            engine.tensor_tensor(
                out=z_part.rearrange("p (c i) t -> p c t i", i=RUN),
                in0=product[g][:, :, cols].rearrange("p t (c i) -> p c t i", i=RUN),
                in1=inter[g][:, :, cols].rearrange("p t (c i) -> p c t i", i=RUN),
                op=ADD,
            )

        def new_z():
            z_grouped = work.tile([P, BANK, PACK], BF16, align_bytes=64, tag="z", bufs=1)
            z_codes = work.tile([P, BANK], U32, align_bytes=64, bufs=3)
            z_scales = work.tile([P, BANK], U8, align_bytes=64, bufs=3)
            return z_grouped, z_codes, z_scales

        def quantise_z(z, start, cols):
            nc.vector.quantize_mx(
                out=z[1][:, start : start + cols].bitcast(FP8X4),
                scales=z[2][:, start : start + cols],
                in_=z[0][:, start : start + cols, :].rearrange("p b t -> p (b t)"),
            )

        def place(g, first_chunk, z, start, cols):
            for c in range(cols // P):
                z_place[g, first_chunk + c] = (z[1], z[2], slice(start + c * P, start + (c + 1) * P))

        def head(g, h, pool):
            bank = pool.tile([P, 2, V], F32, tag="bank")
            for c in range(2):
                codes, scales, cols = z_place[g, 2 * h + c]
                nc.tensor.matmul_mx(
                    out=bank[:, c, :],
                    lhsT=codes[:, cols].bitcast(FP8X4),
                    lhsT_scale=scales[:, cols],
                    rhs=wo_q[0][:].bitcast(FP8X4),
                    rhs_scale=wo_q[1][:],
                    start=True,
                    stop=True,
                )
            out_sb = work.tile([P, 2, V], F32, bufs=4, tag="out")
            nc.vector.tensor_tensor(
                out=out_sb[:], in0=bank[:], in1=bout_bf[:].unsqueeze(1).to_broadcast([P, 2, V]), op=ADD
            )
            nc.sync.dma_start(out=group_rows(out, g)[:, 2 * h : 2 * h + 2, :], in_=out_sb[:])

        def head_products_by_scalar(g):
            for c in range(V // P):
                bank = psum_y.tile([P, BANK], F32, tag="bank")
                codes, scales = z_place[g, 0][0:2]
                nc.tensor.matmul_mx(
                    out=bank[:],
                    lhsT=wo_q[0][:, c * P : (c + 1) * P].bitcast(FP8X4),
                    lhsT_scale=wo_q[1][:, c * P : (c + 1) * P],
                    rhs=codes[:, 0:BANK].bitcast(FP8X4),
                    rhs_scale=scales[:, 0:BANK],
                    start=True,
                    stop=True,
                )
                nc.scalar.activation(
                    out=out_t[:, c, :], in_=bank[:], func=IDENTITY, bias=bo_cols[:, c : c + 1], scale=1.0
                )

        def head_back_by_scalar(g):
            for h, pool in ((0, psum_y), (1, psum_y)):
                bank = pool.tile([P, 2, V], F32, tag="bank")
                for j in range(2):
                    for c in range(V // P):
                        nc.tensor.transpose(
                            bank[:, j, c * P : (c + 1) * P],
                            out_t[:, c, (2 * h + j) * P : (2 * h + j + 1) * P],
                            ident[:],
                        )
                out_sb = work.tile([P, 2, V], F32, bufs=4, tag="out")
                nc.scalar.copy(out=out_sb[:], in_=bank[:])
                nc.sync.dma_start(out=group_rows(out, g)[:, 2 * h : 2 * h + 2, :], in_=out_sb[:])

        def last_head(g):
            for c, pool in ((0, psum_y), (1, psum_first)):
                bank = pool.tile([P, V], F32, tag="bank")
                codes, scales, cols = z_place[g, c]
                nc.tensor.matmul_mx(
                    out=bank[:],
                    lhsT=codes[:, cols].bitcast(FP8X4),
                    lhsT_scale=scales[:, cols],
                    rhs=wo_q[0][:].bitcast(FP8X4),
                    rhs_scale=wo_q[1][:],
                    start=True,
                    stop=True,
                )
                out_sb = work.tile([P, V], F32, tag="last_out")
                nc.vector.tensor_tensor(out=out_sb[:], in0=bank[:], in1=bout_bf[:], op=ADD)
                nc.sync.dma_start(out=group_rows(out, g)[:, c, :], in_=out_sb[:])

        def start_group(g):
            second[g] = work.tile([P, PACK, SIZES[g]], F32, tag="second", name="second")
            inter[g] = work.tile([P, PACK, SIZES[g]], F32, tag="inter", name="inter", bufs=3)

        def copy_pair(grouped, pair, words, copy_out):
            copy_out(
                out=grouped[:].bitcast(F32).rearrange("p (c u) -> p c u", u=2)[:, pair * 2 * P : (pair + 1) * 2 * P, :],
                in_=words[:].rearrange("p u c -> p c u"),
            )

        def y_words(g, pair):
            words = psum_y.tile([P, 2, 2 * P], F32, tag="bank")
            for c in range(2):
                for u in range(2):
                    nc.tensor.transpose(
                        words[:, u, c * P : (c + 1) * P],
                        y_sb[g][:, 2 * pair + c, :].bitcast(F32)[:, u * P : (u + 1) * P],
                        ident[:],
                    )
            return words

        def regroup_y(g, pair, copy_out):
            if pair == 0:
                y_grouped[g] = new_grouped(SIZES[g])
            regroup_pair(psum_y, y_grouped[g], pair, y_sb[g], 2 * pair, copy_out)

        def quantise_y(g):
            y_q[g] = new_quantised(SIZES[g], "y%d" % g)
            quantise(y_q[g], y_grouped[g], 0, SIZES[g])

        y_grouped, y_q, second, inter, first_banks = {}, {}, {}, {}, {}
        product, z_place = {}, {}
        by_scalar, by_vector = nc.scalar.copy, nc.vector.tensor_copy

        def second_of(g, ts):
            relu_of_product(g, ws_q, bs_bf, second[g], ts)

        def inter_of(g, ts):
            relu_of_product(g, wi_q, bi_bf, inter[g], ts)

        ws_grouped, ws_q = new_grouped(K), new_quantised(K, "ws")
        wi_grouped = keep.tile([P, K * PACK], BF16, align_bytes=64)
        wi_q = new_quantised(K, "wi")
        start_group(0)
        regroup_y(0, 0, by_vector)
        keep_warm(STAY_WARM)
        regroup_pair(psum_first, ws_grouped, 0, ws_sb[0], 0, by_scalar)
        quantise_y(0)
        keep_warm(STAY_WARM)
        regroup_pair(psum_first, ws_grouped, 1, ws_sb[1], 0, by_scalar)
        quantise(ws_q, ws_grouped, 0, 2 * P)
        b_words = psum_acc.tile([P, P], F32, tag="acc")
        nc.tensor.transpose(b_words[:], b_rows[:].bitcast(F32), ident[:])
        b_cols = keep.tile([P, 2 * PACK], BF16)
        nc.vector.tensor_copy(out=b_cols[:].bitcast(F32), in_=b_words[:, 0:PACK])
        bs_bf, bi_bf = b_cols[:, 0:PACK], b_cols[:, PACK : 2 * PACK]
        keep_warm(STAY_WARM)
        regroup_pair(psum_y, wi_grouped, 0, wi_sb[0], 0, by_scalar)
        quantise(ws_q, ws_grouped, 2 * P, 2 * P)
        regroup_pair(psum_y, wi_grouped, 1, wi_sb[1], 0, by_vector)
        second_of(0, range(PACK))
        quantise(wi_q, wi_grouped, 0, K)
        regroup_y(1, 0, by_vector)
        regroup_y(1, 1, by_scalar)
        quantise_y(1)
        first_words(0, 0)
        inter_of(0, range(PACK))
        times_first(0, 0)
        bout_bank = psum_acc.tile([P, V], F32, tag="acc")
        nc.tensor.matmul(bout_bank[:], lhsT=ones[:], rhs=bout_row[:], start=True, stop=True)
        bout_bf = keep.tile([P, V], BF16)
        nc.vector.tensor_copy(out=bout_bf[:], in_=bout_bank[:])

        start_group(1)
        z = new_z()
        plus_inter(nc.gpsimd, 0, slice(0, SIZES[0]), z[0][:, 0 : SIZES[0], :])
        second_of(1, (0, 1))
        regroup_y(2, 0, by_vector)
        first_words(1, 0)
        second_of(1, (2, 3))
        times_first(1, 0)
        wo_grouped, wo_q = new_grouped(V), new_quantised(V, "wo")
        regroup_pair(psum_y, wo_grouped, 0, wo_sb, 0, by_vector)
        regroup_y(2, 1, by_scalar)
        first_words(1, 1)
        inter_of(1, (0, 1))
        times_first(1, 1)
        quantise_y(2)
        regroup_y(3, 0, by_vector)
        inter_of(1, (2, 3))
        regroup_y(3, 1, by_vector)
        quantise(wo_q, wo_grouped, 0, V)
        quantise_z(z, 0, SIZES[0])
        place(0, 0, z, 0, SIZES[0])
        quantise_y(3)
        first_words(2, 0)

        bo_bank = psum_acc.tile([P, P], F32, tag="acc")
        nc.tensor.matmul(bo_bank[:], lhsT=bo_rows[:], rhs=ident_bf[:], start=True, stop=True)
        nc.scalar.copy(out=bo_cols[:], in_=bo_bank[:, 0 : V // P])

        for r in range(2, N_GROUPS):
            start_group(r)
            second_of(r, range(PACK))
            if SIZES[r] == BANK:
                first_words(r, 1)
            z = new_z()
            n = SIZES[r - 1]
            share = SHARE if r < N_GROUPS - 1 else SHARE_LAST
            plus_inter(nc.gpsimd, r - 1, slice(share, n), z[0][:, share:n, :])
            for part in parts(r):
                times_first(r, part)
            if r + 2 < N_GROUPS:
                regroup_y(r + 2, 0, by_scalar)
            if r + 2 < N_GROUPS and SIZES[r + 2] == BANK:
                regroup_y(r + 2, 1, by_vector if r == 2 else by_scalar)
            inter_of(r, (0, 1))
            if r < N_GROUPS - 1:
                head(r - 2, 0, psum_y)
            inter_of(r, (2, 3))
            if SIZES[r - 2] == BANK and r < N_GROUPS - 1:
                head(r - 2, 1, psum_y)
            if r == N_GROUPS - 1:
                head_products_by_scalar(r - 2)
            if r + 1 < N_GROUPS:
                first_words(r + 1, 0)
            plus_inter(nc.vector, r - 1, slice(0, share), z[0][:, 0:share, :])
            if r + 2 < N_GROUPS:
                quantise_y(r + 2)
            quantise_z(z, 0, n)
            place(r - 1, 0, z, 0, n)

        last = N_GROUPS - 1
        z = new_z()
        n = SIZES[last]
        head_back_by_scalar(last - 2)
        plus_inter(nc.vector, last, slice(0, n), z[0][:, 0:n, :])
        head(last - 1, 0, psum_y)
        quantise_z(z, 0, n)
        place(last, 0, z, 0, n)
        if SIZES[last - 1] == BANK:
            head(last - 1, 1, psum_y)
        last_head(last)
